import numpy as np
import ml_dtypes


def mxq(x, axis, fmt="e4m3"):
    dtype, down = {"e4m3": (ml_dtypes.float8_e4m3fn, 7), "e5m2": (ml_dtypes.float8_e5m2, 14)}[fmt]
    v = np.moveaxis(np.asarray(x, np.float32).astype(ml_dtypes.bfloat16).astype(np.float64), axis, -1)
    blocks = v.reshape(v.shape[:-1] + (-1, 32))
    amax = np.abs(blocks).max(-1, keepdims=True)
    byte = np.maximum(np.where(amax > 0, np.frexp(amax)[1] - 1 + 127, 0) - down, 1)
    scale = np.exp2(byte - 127.0)
    codes = (blocks / scale).astype(np.float32).astype(dtype).astype(np.float64)
    return np.moveaxis((codes * scale).reshape(v.shape), -1, axis)


WIDE = False


def mx_kscale(k):
    if not WIDE:
        return np.ones(k)
    levels = np.array([10, -10, 5, -5, 0])
    a = np.random.permutation(np.resize(levels, k // 512 * 4)).reshape(k // 512, 4)
    idx = np.arange(k)
    return np.exp2(a[idx // 512, idx % 128 // 32])


BF16 = ml_dtypes.bfloat16


def bf(x):
    return np.asarray(x, np.float32).astype(BF16)


def f64(x):
    return np.asarray(x).astype(np.float64)


M, DI, N, DO, TS = 256, 1024, 2048, 1024, 3
DENSITY = 0.25


def setup_inputs():
    k = mx_kscale(DI)
    m = (np.random.uniform(size=(N, N)) < DENSITY).astype(np.float64)
    return {'x': bf(np.random.standard_normal((M, DI)) * k),
            'W_in': bf(np.random.standard_normal((N, DI)) / np.sqrt(DI) / k),
            'b_in': bf(np.random.standard_normal(N) * 0.3),
            'weights': bf(np.random.standard_normal((N, N)) * 1.5 / np.sqrt(DENSITY * N)),
            'J': bf(np.random.standard_normal((N, N)) * 2.0 / np.sqrt(DENSITY * N)),
            'theta': bf(np.random.uniform(size=N) * 1.0 + 0.25),
            'lam': bf(0.35 + 0.05 * np.random.standard_normal(1)),
            'mask': bf(m * (1.0 - np.eye(N))),
            'noise_raw': bf(np.random.standard_normal((M, N)) * 2.5)}


def reference(x, W_in, b_in, weights, J, theta, lam, mask, noise_raw):
    state = (mxq(f64(x), 1, 'e4m3') @ mxq(f64(W_in), 1, 'e4m3').T) + f64(b_in)
    eff_w = f64(weights) * f64(mask)
    J_m = f64(J) * f64(mask)
    T = np.abs(np.sin(2.0 * f64(theta)))
    signal = mxq(state, 1, 'e4m3') @ mxq(eff_w, 0, 'e4m3')
    s = np.tanh(state)
    delta = (mxq(s, 1, 'e4m3') @ mxq(J_m, 0, 'e4m3')) * s
    noise = f64(noise_raw) * T * 0.1
    return np.tanh(signal + f64(lam) * delta + noise)

@@ -1,0 +1,262 @@
+from contextlib import ExitStack
+import math
+
+import concourse.bass as bass
+import concourse.mybir as mybir
+import concourse.tile as tile
+from concourse.masks import make_identity
+
+F32 = mybir.dt.float32
+BF16 = mybir.dt.bfloat16
+U32 = mybir.dt.uint32
+U8 = mybir.dt.uint8
+I32 = mybir.dt.int32
+FP8X4 = mybir.dt.float8_e4m3fn_x4
+ACT = mybir.ActivationFunctionType
+ALU = mybir.AluOpType
+
+P = 128
+M, DI, N = 256, 1024, 2048
+FLOPS = 2 * M * DI * N + 2 * 2 * M * N * N
+
+PI_HI = 3.140625
+PI_LO = math.pi - PI_HI
+
+
+def tile_brainquantumlayer_pa_kernel(
+    tc, x, W_in, b_in, weights, J, theta, lam, mask, noise_raw, out
+):
+    nc = tc.nc
+    with ExitStack() as ctx:
+        const = ctx.enter_context(tc.tile_pool(name="const", bufs=1))
+        early = ctx.enter_context(tc.tile_pool(name="early", bufs=2))
+        stream = ctx.enter_context(tc.tile_pool(name="stream", bufs=2))
+        work = ctx.enter_context(tc.tile_pool(name="work", bufs=3))
+        psum = ctx.enter_context(tc.psum_pool(name="psum", bufs=1))
+
+        def bank(i, shape, name):
+            return psum.tile(shape, F32, tag="bank%d" % i, name=name)
+
+        ident = const.tile([P, P], F32, name="ident")
+        make_identity(nc, ident[:])
+
+        th_b = const.tile([P, 4, 4], BF16, name="th_b")
+        b_b = const.tile([P, 4, 4], BF16, name="b_b")
+        lam_b = const.tile([P, 1], BF16, name="lam_b")
+        with nc.allow_non_contiguous_dma(reason="three small vectors, 8-byte runs"):
+            nc.scalar.dma_start(out=th_b[:], in_=theta.rearrange("(g p j) -> p g j", g=4, j=4))
+            nc.scalar.dma_start(out=b_b[:], in_=b_in.rearrange("(g p j) -> p g j", g=4, j=4))
+            nc.scalar.dma_start(out=lam_b[:], in_=lam.partition_broadcast(P))
+
+        x_sb = early.tile([P, 2, DI], BF16, name="x_sb", tag="win", bufs=3)
+        nc.sync.dma_start(out=x_sb[:], in_=x.rearrange("(t p) k -> p t k", p=P))
+
+        th_flat = th_b[:].rearrange("p g j -> p (g j)")
+        tq = const.tile([P, 16], F32, name="tq")
+        nc.vector.tensor_scalar_mul(out=tq[:], in0=th_flat, scalar1=2.0 / math.pi)
+        ni = const.tile([P, 16], I32, name="ni")
+        nc.vector.tensor_copy(out=ni[:], in_=tq[:])
+        nf = const.tile([P, 16], F32, name="nf")
+        nc.vector.tensor_copy(out=nf[:], in_=ni[:])
+        y2 = const.tile([P, 16], F32, name="y2")
+        nc.vector.tensor_scalar_mul(out=y2[:], in0=th_flat, scalar1=2.0)
+        r1 = const.tile([P, 16], F32, name="r1")
+        nc.vector.scalar_tensor_tensor(
+            out=r1[:], in0=nf[:], scalar=-PI_HI, in1=y2[:], op0=ALU.mult, op1=ALU.add
+        )
+        r2 = const.tile([P, 16], F32, name="r2")
+        nc.vector.scalar_tensor_tensor(
+            out=r2[:], in0=nf[:], scalar=-PI_LO, in1=r1[:], op0=ALU.mult, op1=ALU.add
+        )
+        sn = const.tile([P, 16], F32, name="sn")
+        nc.scalar.activation(out=sn[:], in_=r2[:], func=ACT.Sin)
+        s01 = const.tile([P, 16], F32, name="s01")
+        nc.vector.tensor_scalar_mul(out=s01[:], in0=sn[:], scalar1=0.1)
+        t_f = const.tile([P, 16], F32, name="t_f")
+        nc.vector.scalar_tensor_tensor(
+            out=t_f[:], in0=s01[:], scalar=-1.0, in1=s01[:], op0=ALU.mult, op1=ALU.max
+        )
+        bias_f = const.tile([P, 16], F32, name="bias_f")
+        nc.vector.tensor_copy(out=bias_f[:], in_=b_b[:].rearrange("p g j -> p (g j)"))
+        lam_f = const.tile([P, 1], F32, name="lam_f")
+        nc.vector.tensor_copy(out=lam_f[:], in_=lam_b[:])
+
+        tr_count = [0]
+
+        def transpose_words(src_f32, dst_f32, on_vector):
+            ps = bank(tr_count[0] % 3, [P, 4, P], "tr_ps")
+            tr_count[0] += 1
+            for q in range(4):
+                nc.tensor.transpose(ps[:, q, :], src_f32[:, P * q : P * (q + 1)], ident[:])
+            view = ps[:].rearrange("p (c u) r -> p c r u", u=2)
+            if on_vector:
+                nc.vector.tensor_copy(out=dst_f32, in_=view)
+            else:
+                nc.scalar.copy(out=dst_f32, in_=view)
+
+        xg = early.tile([P, 2, 2 * P, 4], BF16, name="xg", tag="wgrp", align_bytes=64)
+        for t in range(2):
+            transpose_words(
+                x_sb[:].bitcast(F32)[:, t, :],
+                xg[:].bitcast(F32)[:, :, P * t : P * (t + 1), :],
+                t == 0,
+            )
+        xq = const.tile([P, 2, 2 * P], U32, name="xq", align_bytes=64)
+        xqs = const.tile([P, 2, 2 * P], U8, name="xqs", align_bytes=64)
+        nc.vector.quantize_mx(
+            out=xq[:].rearrange("p c w -> p (c w)").bitcast(FP8X4),
+            scales=xqs[:].rearrange("p c w -> p (c w)"),
+            in_=xg[:].rearrange("p c w t -> p (c w t)"),
+        )
+
+        stq = const.tile([P, 4, 2, M], U32, name="stq", align_bytes=64)
+        stqs = const.tile([P, 4, 2, M], U8, name="stqs", align_bytes=64)
+        s_sb = const.tile([P, 2, N], F32, name="s_sb")
+        nz = const.tile([P, 2, N], F32, name="nz")
+
+        for g in range(4):
+            win = early.tile([P, 4, DI], BF16, name="win", tag="win", bufs=3)
+            nc.sync.dma_start(
+                out=win[:],
+                in_=W_in[512 * g : 512 * (g + 1), :].rearrange("(p j) k -> p j k", j=4),
+            )
+            wgrp = early.tile([P, 2, 512, 4], BF16, name="wgrp", tag="wgrp", align_bytes=64)
+            for j in range(4):
+                transpose_words(
+                    win[:].bitcast(F32)[:, j, :],
+                    wgrp[:].bitcast(F32)[:, :, P * j : P * (j + 1), :],
+                    j % 2 == 1,
+                )
+            wq = early.tile([P, 2, 512], U32, name="wq", align_bytes=64)
+            wqs = early.tile([P, 2, 512], U8, name="wqs", align_bytes=64)
+            nc.vector.quantize_mx(
+                out=wq[:].rearrange("p c w -> p (c w)").bitcast(FP8X4),
+                scales=wqs[:].rearrange("p c w -> p (c w)"),
+                in_=wgrp[:].rearrange("p c w t -> p (c w t)"),
+            )
+            stb = early.tile([P, 4, M], BF16, name="stb")
+            sT = early.tile([P, 4, M], F32, name="sT")
+            for half in range(2):
+                st = bank(3 + half, [P, 2, M], "st_ps")
+                for jj in range(2):
+                    j = 2 * half + jj
+                    for c in range(2):
+                        nc.tensor.matmul_mx(
+                            out=st[:, jj, :],
+                            lhsT=wq[:, c, P * j : P * (j + 1)].bitcast(FP8X4),
+                            lhsT_scale=wqs[:, c, P * j : P * (j + 1)],
+                            rhs=xq[:, c, :].bitcast(FP8X4),
+                            rhs_scale=xqs[:, c, :],
+                            start=(c == 0),
+                            stop=(c == 1),
+                        )
+                for jj in range(2):
+                    j = 2 * half + jj
+                    b_col = bias_f[:, 4 * g + j : 4 * g + j + 1]
+                    nc.scalar.activation(
+                        out=stb[:, j, :], in_=st[:, jj, :], func=ACT.Identity, bias=b_col
+                    )
+                    nc.scalar.activation(
+                        out=sT[:, j, :], in_=st[:, jj, :], func=ACT.Tanh, bias=b_col
+                    )
+            gst = early.tile([P, 2, M, 4], BF16, name="gst", align_bytes=64)
+            nc.vector.tensor_copy(out=gst[:, 0], in_=stb[:].rearrange("p j m -> p m j"))
+            nc.vector.tensor_copy(out=gst[:, 1], in_=sT[:].rearrange("p j m -> p m j"))
+            nc.vector.quantize_mx(
+                out=stq[:, g].rearrange("p a m -> p (a m)").bitcast(FP8X4),
+                scales=stqs[:, g].rearrange("p a m -> p (a m)"),
+                in_=gst[:].rearrange("p a m j -> p (a m j)"),
+            )
+            for mt in range(2):
+                sp = bank(5 + mt, [P, 4, P], "sp_ps")
+                for j in range(4):
+                    nc.tensor.transpose(sp[:, j, :], sT[:, j, P * mt : P * (mt + 1)], ident[:])
+                nc.scalar.activation(
+                    out=s_sb[:, mt, 512 * g : 512 * (g + 1)].rearrange("p (r j) -> p r j", j=4),
+                    in_=sp[:].rearrange("p j r -> p r j"),
+                    func=ACT.Copy,
+                    scale=lam_f[:, 0:1],
+                )
+
+        noise = early.tile([P, 2, N], BF16, name="noise", bufs=1)
+        nc.sync.dma_start(out=noise[:], in_=noise_raw.rearrange("(t p) n -> p t n", p=P))
+        for g in range(4):
+            tb = bank(7, [P, 4, P], "tb_ps")
+            for j in range(4):
+                nc.tensor.matmul(
+                    out=tb[:, j, :],
+                    lhsT=t_f[:, 4 * g + j : 4 * g + j + 1].to_broadcast([P, P]),
+                    rhs=ident[:],
+                    start=True,
+                    stop=True,
+                )
+            for mt in range(2):
+                blk = slice(512 * g, 512 * (g + 1))
+                nc.vector.tensor_tensor(
+                    out=nz[:, mt, blk].rearrange("p (r j) -> p r j", j=4),
+                    in0=noise[:, mt, blk].rearrange("p (r j) -> p r j", j=4),
+                    in1=tb[:].rearrange("p j r -> p r j"),
+                    op=ALU.mult,
+                )
+
+        for h in range(2):
+            acc = {}
+            for g in range(4):
+                rows = slice(512 * g, 512 * (g + 1))
+                cols = slice(1024 * h, 1024 * (h + 1))
+                m_t = stream.tile([P, 4, 1024], BF16, name="m_t")
+                nc.sync.dma_start(out=m_t[:], in_=mask[rows, cols].rearrange("(p j) n -> p j n", j=4))
+                j_t = stream.tile([P, 4, 1024], BF16, name="j_t")
+                nc.sync.dma_start(out=j_t[:], in_=J[rows, cols].rearrange("(p j) n -> p j n", j=4))
+                w_t = stream.tile([P, 4, 1024], BF16, name="w_t")
+                nc.sync.dma_start(out=w_t[:], in_=weights[rows, cols].rearrange("(p j) n -> p j n", j=4))
+                for a, src in ((1, j_t), (0, w_t)):
+                    for nb in range(2):
+                        c = slice(512 * nb, 512 * (nb + 1))
+                        prod = work.tile([P, 4, 512], BF16, name="prod")
+                        nc.vector.tensor_tensor(
+                            out=prod[:], in0=src[:, :, c], in1=m_t[:, :, c], op=ALU.mult
+                        )
+                        grp = work.tile([P, 512, 4], BF16, name="grp", align_bytes=64)
+                        nc.scalar.copy(
+                            out=grp[:].rearrange("p (c i) t -> p c t i", i=4),
+                            in_=prod[:].rearrange("p t (c i) -> p c t i", i=4),
+                        )
+                        cod = work.tile([P, 512], U32, name="cod", bufs=5, align_bytes=64)
+                        scl = work.tile([P, 512], U8, name="scl", bufs=5, align_bytes=64)
+                        nc.vector.quantize_mx(
+                            out=cod[:].bitcast(FP8X4),
+                            scales=scl[:],
+                            in_=grp[:].rearrange("p n t -> p (n t)"),
+                        )
+                        ncols = slice(1024 * h + 512 * nb, 1024 * h + 512 * (nb + 1))
+                        for mt in range(2):
+                            if g == 0:
+                                acc[(a, mt, nb)] = bank(4 * (1 - a) + 2 * mt + nb, [P, 512], "acc")
+                            nc.tensor.matmul_mx(
+                                out=acc[(a, mt, nb)][:],
+                                lhsT=stq[:, g, a, P * mt : P * (mt + 1)].bitcast(FP8X4),
+                                lhsT_scale=stqs[:, g, a, P * mt : P * (mt + 1)],
+                                rhs=cod[:].bitcast(FP8X4),
+                                rhs_scale=scl[:],
+                                start=(g == 0),
+                                stop=(g == 3),
+                            )
+                        if g == 3:
+                            for mt in range(2):
+                                if a == 1:
+                                    vt = work.tile([P, 512], F32, name="vt", bufs=2)
+                                    nc.vector.tensor_tensor(
+                                        out=vt[:], in0=acc[(a, mt, nb)][:], in1=s_sb[:, mt, ncols], op=ALU.mult
+                                    )
+                                    nc.vector.tensor_tensor(
+                                        out=nz[:, mt, ncols], in0=vt[:], in1=nz[:, mt, ncols], op=ALU.add
+                                    )
+                                else:
+                                    pre = work.tile([P, 512], F32, name="pre", bufs=2)
+                                    nc.vector.tensor_tensor(
+                                        out=pre[:], in0=acc[(a, mt, nb)][:], in1=nz[:, mt, ncols], op=ALU.add
+                                    )
+                                    o_t = work.tile([P, 512], F32, name="o_t")
+                                    nc.scalar.activation(out=o_t[:], in_=pre[:], func=ACT.Tanh)
+                                    nc.sync.dma_start(out=out[P * mt : P * (mt + 1), ncols], in_=o_t[:])

@@ -1,9 +1,7 @@
 from contextlib import ExitStack
 import math
 
-import concourse.bass as bass
 import concourse.mybir as mybir
-import concourse.tile as tile
 from concourse.masks import make_identity
 
 F32 = mybir.dt.float32
@@ -22,6 +20,9 @@ FLOPS = 2 * M * DI * N + 2 * 2 * M * N * N
 PI_HI = 3.140625
 PI_LO = math.pi - PI_HI
 
+ACC_BANKS = (4, 5, 6, 2, 3)
+VECTOR_COLS = 256
+
 
 def tile_brainquantumlayer_pa_kernel(
     tc, x, W_in, b_in, weights, J, theta, lam, mask, noise_raw, out
@@ -34,32 +35,50 @@ def tile_brainquantumlayer_pa_kernel(
         work = ctx.enter_context(tc.tile_pool(name="work", bufs=3))
         psum = ctx.enter_context(tc.psum_pool(name="psum", bufs=1))
 
-        def bank(i, shape, name):
-            return psum.tile(shape, F32, tag="bank%d" % i, name=name)
-
-        ident = const.tile([P, P], F32, name="ident")
-        make_identity(nc, ident[:])
-
-        th_b = const.tile([P, 4, 4], BF16, name="th_b")
-        b_b = const.tile([P, 4, 4], BF16, name="b_b")
-        lam_b = const.tile([P, 1], BF16, name="lam_b")
-        with nc.allow_non_contiguous_dma(reason="three small vectors, 8-byte runs"):
-            nc.scalar.dma_start(out=th_b[:], in_=theta.rearrange("(g p j) -> p g j", g=4, j=4))
-            nc.scalar.dma_start(out=b_b[:], in_=b_in.rearrange("(g p j) -> p g j", g=4, j=4))
-            nc.scalar.dma_start(out=lam_b[:], in_=lam.partition_broadcast(P))
+        def bank(i, shape, name, dtype=F32):
+            return psum.tile(shape, dtype, tag="bank%d" % i, name=name)
 
         x_sb = early.tile([P, 2, DI], BF16, name="x_sb", tag="win", bufs=3)
         nc.sync.dma_start(out=x_sb[:], in_=x.rearrange("(t p) k -> p t k", p=P))
+        wins = {}
 
-        th_flat = th_b[:].rearrange("p g j -> p (g j)")
+        def load_win(g):
+            win = early.tile([P, 4, DI], BF16, name="win", tag="win", bufs=3)
+            for t in range(4):
+                r0 = 512 * g + P * t
+                nc.sync.dma_start(out=win[:, t, :], in_=W_in[r0 : r0 + P, :])
+            wins[g] = win
+
+        load_win(0)
+        load_win(1)
+
+        ident = const.tile([P, P], F32, name="ident")
+        make_identity(nc, ident[:])
+        ident_b = const.tile([P, P], BF16, name="ident_b")
+        make_identity(nc, ident_b[:])
+
+        vecs = const.tile([P, P], BF16, name="vecs")
+        nc.vector.memset(vecs[:], 0.0)
+        nc.scalar.dma_start(out=vecs[0:16, :], in_=b_in.rearrange("(i p) -> i p", p=P))
+        nc.scalar.dma_start(out=vecs[16:32, :], in_=theta.rearrange("(i p) -> i p", p=P))
+        lam_b = const.tile([P, 1], BF16, name="lam_b")
+        nc.scalar.dma_start(out=lam_b[:], in_=lam.partition_broadcast(P))
+
+        vps = bank(0, [P, P], "vps", BF16)
+        nc.tensor.transpose(vps[:], vecs[:], ident_b[:])
+        vec_f = const.tile([P, 32], F32, name="vec_f")
+        nc.vector.tensor_copy(out=vec_f[:], in_=vps[:, 0:32])
+        bias_f = vec_f[:, 0:16]
+        th_f = vec_f[:, 16:32]
+
         tq = const.tile([P, 16], F32, name="tq")
-        nc.vector.tensor_scalar_mul(out=tq[:], in0=th_flat, scalar1=2.0 / math.pi)
+        nc.vector.tensor_scalar_mul(out=tq[:], in0=th_f, scalar1=2.0 / math.pi)
         ni = const.tile([P, 16], I32, name="ni")
         nc.vector.tensor_copy(out=ni[:], in_=tq[:])
         nf = const.tile([P, 16], F32, name="nf")
         nc.vector.tensor_copy(out=nf[:], in_=ni[:])
         y2 = const.tile([P, 16], F32, name="y2")
-        nc.vector.tensor_scalar_mul(out=y2[:], in0=th_flat, scalar1=2.0)
+        nc.vector.tensor_scalar_mul(out=y2[:], in0=th_f, scalar1=2.0)
         r1 = const.tile([P, 16], F32, name="r1")
         nc.vector.scalar_tensor_tensor(
             out=r1[:], in0=nf[:], scalar=-PI_HI, in1=y2[:], op0=ALU.mult, op1=ALU.add
@@ -76,30 +95,24 @@ def tile_brainquantumlayer_pa_kernel(
         nc.vector.scalar_tensor_tensor(
             out=t_f[:], in0=s01[:], scalar=-1.0, in1=s01[:], op0=ALU.mult, op1=ALU.max
         )
-        bias_f = const.tile([P, 16], F32, name="bias_f")
-        nc.vector.tensor_copy(out=bias_f[:], in_=b_b[:].rearrange("p g j -> p (g j)"))
         lam_f = const.tile([P, 1], F32, name="lam_f")
         nc.vector.tensor_copy(out=lam_f[:], in_=lam_b[:])
 
         tr_count = [0]
 
-        def transpose_words(src_f32, dst_f32, on_vector):
-            ps = bank(tr_count[0] % 3, [P, 4, P], "tr_ps")
+        def transpose_words(src_f32, dst_f32):
+            ps = bank(tr_count[0] % 2, [P, 4, P], "tr_ps")
             tr_count[0] += 1
             for q in range(4):
                 nc.tensor.transpose(ps[:, q, :], src_f32[:, P * q : P * (q + 1)], ident[:])
             view = ps[:].rearrange("p (c u) r -> p c r u", u=2)
-            if on_vector:
-                nc.vector.tensor_copy(out=dst_f32, in_=view)
-            else:
-                nc.scalar.copy(out=dst_f32, in_=view)
+            nc.scalar.copy(out=dst_f32, in_=view)
 
         xg = early.tile([P, 2, 2 * P, 4], BF16, name="xg", tag="wgrp", align_bytes=64)
         for t in range(2):
             transpose_words(
                 x_sb[:].bitcast(F32)[:, t, :],
                 xg[:].bitcast(F32)[:, :, P * t : P * (t + 1), :],
-                t == 0,
             )
         xq = const.tile([P, 2, 2 * P], U32, name="xq", align_bytes=64)
         xqs = const.tile([P, 2, 2 * P], U8, name="xqs", align_bytes=64)
@@ -111,22 +124,23 @@ def tile_brainquantumlayer_pa_kernel(
 
         stq = const.tile([P, 4, 2, M], U32, name="stq", align_bytes=64)
         stqs = const.tile([P, 4, 2, M], U8, name="stqs", align_bytes=64)
-        s_sb = const.tile([P, 2, N], F32, name="s_sb")
-        nz = const.tile([P, 2, N], F32, name="nz")
+        sT = const.tile([P, 16, M], F32, name="sT")
 
-        for g in range(4):
-            win = early.tile([P, 4, DI], BF16, name="win", tag="win", bufs=3)
-            nc.sync.dma_start(
-                out=win[:],
-                in_=W_in[512 * g : 512 * (g + 1), :].rearrange("(p j) k -> p j k", j=4),
-            )
+        wgrps = {}
+        stbs = {}
+
+        def stage_a(g):
+            win = wins[g]
             wgrp = early.tile([P, 2, 512, 4], BF16, name="wgrp", tag="wgrp", align_bytes=64)
-            for j in range(4):
+            wgrps[g] = wgrp
+            for t in range(4):
                 transpose_words(
-                    win[:].bitcast(F32)[:, j, :],
-                    wgrp[:].bitcast(F32)[:, :, P * j : P * (j + 1), :],
-                    j % 2 == 1,
+                    win[:].bitcast(F32)[:, t, :],
+                    wgrp[:].bitcast(F32)[:, :, P * t : P * (t + 1), :],
                 )
+
+        def stage_b(g):
+            wgrp = wgrps[g]
             wq = early.tile([P, 2, 512], U32, name="wq", align_bytes=64)
             wqs = early.tile([P, 2, 512], U8, name="wqs", align_bytes=64)
             nc.vector.quantize_mx(
@@ -135,128 +149,205 @@ def tile_brainquantumlayer_pa_kernel(
                 in_=wgrp[:].rearrange("p c w t -> p (c w t)"),
             )
             stb = early.tile([P, 4, M], BF16, name="stb")
-            sT = early.tile([P, 4, M], F32, name="sT")
+            stbs[g] = stb
             for half in range(2):
-                st = bank(3 + half, [P, 2, M], "st_ps")
-                for jj in range(2):
-                    j = 2 * half + jj
+                st = bank(2 + half, [P, 2, M], "st_ps")
+                for tt in range(2):
+                    t = 2 * half + tt
                     for c in range(2):
                         nc.tensor.matmul_mx(
-                            out=st[:, jj, :],
-                            lhsT=wq[:, c, P * j : P * (j + 1)].bitcast(FP8X4),
-                            lhsT_scale=wqs[:, c, P * j : P * (j + 1)],
+                            out=st[:, tt, :],
+                            lhsT=wq[:, c, P * t : P * (t + 1)].bitcast(FP8X4),
+                            lhsT_scale=wqs[:, c, P * t : P * (t + 1)],
                             rhs=xq[:, c, :].bitcast(FP8X4),
                             rhs_scale=xqs[:, c, :],
                             start=(c == 0),
                             stop=(c == 1),
                         )
-                for jj in range(2):
-                    j = 2 * half + jj
-                    b_col = bias_f[:, 4 * g + j : 4 * g + j + 1]
+                for tt in range(2):
+                    t = 2 * half + tt
+                    i = 4 * g + t
                     nc.scalar.activation(
-                        out=stb[:, j, :], in_=st[:, jj, :], func=ACT.Identity, bias=b_col
+                        out=stb[:, t, :], in_=st[:, tt, :], func=ACT.Identity, bias=bias_f[:, i : i + 1]
                     )
                     nc.scalar.activation(
-                        out=sT[:, j, :], in_=st[:, jj, :], func=ACT.Tanh, bias=b_col
+                        out=sT[:, i, :], in_=st[:, tt, :], func=ACT.Tanh, bias=bias_f[:, i : i + 1]
                     )
+
+        def stage_c(g):
+            stb = stbs[g]
             gst = early.tile([P, 2, M, 4], BF16, name="gst", align_bytes=64)
-            nc.vector.tensor_copy(out=gst[:, 0], in_=stb[:].rearrange("p j m -> p m j"))
-            nc.vector.tensor_copy(out=gst[:, 1], in_=sT[:].rearrange("p j m -> p m j"))
+            nc.vector.tensor_copy(out=gst[:, 0], in_=stb[:].rearrange("p t m -> p m t"))
+            nc.vector.tensor_copy(
+                out=gst[:, 1], in_=sT[:, 4 * g : 4 * (g + 1), :].rearrange("p t m -> p m t")
+            )
             nc.vector.quantize_mx(
                 out=stq[:, g].rearrange("p a m -> p (a m)").bitcast(FP8X4),
                 scales=stqs[:, g].rearrange("p a m -> p (a m)"),
-                in_=gst[:].rearrange("p a m j -> p (a m j)"),
+                in_=gst[:].rearrange("p a m t -> p (a m t)"),
             )
-            for mt in range(2):
-                sp = bank(5 + mt, [P, 4, P], "sp_ps")
-                for j in range(4):
-                    nc.tensor.transpose(sp[:, j, :], sT[:, j, P * mt : P * (mt + 1)], ident[:])
-                nc.scalar.activation(
-                    out=s_sb[:, mt, 512 * g : 512 * (g + 1)].rearrange("p (r j) -> p r j", j=4),
-                    in_=sp[:].rearrange("p j r -> p r j"),
-                    func=ACT.Copy,
-                    scale=lam_f[:, 0:1],
-                )
 
-        noise = early.tile([P, 2, N], BF16, name="noise", bufs=1)
-        nc.sync.dma_start(out=noise[:], in_=noise_raw.rearrange("(t p) n -> p t n", p=P))
-        for g in range(4):
-            tb = bank(7, [P, 4, P], "tb_ps")
-            for j in range(4):
-                nc.tensor.matmul(
-                    out=tb[:, j, :],
-                    lhsT=t_f[:, 4 * g + j : 4 * g + j + 1].to_broadcast([P, P]),
-                    rhs=ident[:],
-                    start=True,
-                    stop=True,
-                )
-            for mt in range(2):
-                blk = slice(512 * g, 512 * (g + 1))
-                nc.vector.tensor_tensor(
-                    out=nz[:, mt, blk].rearrange("p (r j) -> p r j", j=4),
-                    in0=noise[:, mt, blk].rearrange("p (r j) -> p r j", j=4),
-                    in1=tb[:].rearrange("p j r -> p r j"),
-                    op=ALU.mult,
-                )
+        codes = const.tile([P, 2, 4, 2, 512], U32, name="codes", align_bytes=64)
+        scl = const.tile([P, 2, 4, 2, 512], U8, name="scl", align_bytes=64)
+        noise = const.tile([P, 2, N], BF16, name="noise")
+        sets = {}
+        eps = {}
+        nts = {}
+        acc_count = [0]
 
-        for h in range(2):
-            acc = {}
-            for g in range(4):
-                rows = slice(512 * g, 512 * (g + 1))
-                cols = slice(1024 * h, 1024 * (h + 1))
-                m_t = stream.tile([P, 4, 1024], BF16, name="m_t")
-                nc.sync.dma_start(out=m_t[:], in_=mask[rows, cols].rearrange("(p j) n -> p j n", j=4))
-                j_t = stream.tile([P, 4, 1024], BF16, name="j_t")
-                nc.sync.dma_start(out=j_t[:], in_=J[rows, cols].rearrange("(p j) n -> p j n", j=4))
-                w_t = stream.tile([P, 4, 1024], BF16, name="w_t")
-                nc.sync.dma_start(out=w_t[:], in_=weights[rows, cols].rearrange("(p j) n -> p j n", j=4))
-                for a, src in ((1, j_t), (0, w_t)):
-                    for nb in range(2):
-                        c = slice(512 * nb, 512 * (nb + 1))
-                        prod = work.tile([P, 4, 512], BF16, name="prod")
-                        nc.vector.tensor_tensor(
-                            out=prod[:], in0=src[:, :, c], in1=m_t[:, :, c], op=ALU.mult
+        def load_one(s, kind):
+            h, g = divmod(s, 4)
+            src = {"m": mask, "j": J, "w": weights}[kind]
+            t_in = stream.tile([P, 4, 1024], BF16, name="in_" + kind, tag="in_" + kind)
+            nc.sync.dma_start(
+                out=t_in[:],
+                in_=src[512 * g : 512 * (g + 1), 1024 * h : 1024 * (h + 1)].rearrange(
+                    "(t p) n -> p t n", p=P
+                ),
+            )
+            sets[(s, kind)] = t_in
+
+        accs = {}
+
+        def burst(h, a, nb):
+            i0 = 8 * h + 4 * nb
+            if a == 1:
+                n_t = bank(7, [P, 4, M], "n_t", BF16)
+                nts[(h, nb)] = n_t
+                for c in range(4):
+                    for mt in range(2):
+                        nc.tensor.transpose(
+                            n_t[:, c, P * mt : P * (mt + 1)],
+                            noise[:, mt, P * (i0 + c) : P * (i0 + c + 1)],
+                            ident_b[:],
                         )
-                        grp = work.tile([P, 512, 4], BF16, name="grp", align_bytes=64)
-                        nc.scalar.copy(
-                            out=grp[:].rearrange("p (c i) t -> p c t i", i=4),
-                            in_=prod[:].rearrange("p t (c i) -> p c t i", i=4),
+            for q in range(2):
+                acc = bank(ACC_BANKS[acc_count[0] % 5], [P, 2, M], "acc")
+                acc_count[0] += 1
+                accs[(h, a, nb, q)] = acc
+                for c2 in range(2):
+                    c = 2 * q + c2
+                    for gg in range(4):
+                        nc.tensor.matmul_mx(
+                            out=acc[:, c2, :],
+                            lhsT=codes[:, a, gg, nb, P * c : P * (c + 1)].bitcast(FP8X4),
+                            lhsT_scale=scl[:, a, gg, nb, P * c : P * (c + 1)],
+                            rhs=stq[:, gg, a, :].bitcast(FP8X4),
+                            rhs_scale=stqs[:, gg, a, :],
+                            start=(gg == 0),
+                            stop=(gg == 3),
                         )
-                        cod = work.tile([P, 512], U32, name="cod", bufs=5, align_bytes=64)
-                        scl = work.tile([P, 512], U8, name="scl", bufs=5, align_bytes=64)
-                        nc.vector.quantize_mx(
-                            out=cod[:].bitcast(FP8X4),
-                            scales=scl[:],
-                            in_=grp[:].rearrange("p n t -> p (n t)"),
+
+        def finish(h, a, nb):
+            i0 = 8 * h + 4 * nb
+            if a == 1:
+                eps[(h, nb)] = work.tile([P, 4, M], F32, name="ep", bufs=2)
+            ep = eps[(h, nb)]
+            n_t = nts[(h, nb)]
+            for q in range(2):
+                acc = accs[(h, a, nb, q)]
+                pair = slice(2 * q, 2 * q + 2)
+                if a == 1:
+                    nc.vector.scalar_tensor_tensor(
+                        out=ep[:, pair, :],
+                        in0=acc[:],
+                        scalar=lam_f[:, 0:1],
+                        in1=sT[:, i0 + 2 * q : i0 + 2 * q + 2, :],
+                        op0=ALU.mult,
+                        op1=ALU.mult,
+                    )
+                    for c2 in range(2):
+                        c = 2 * q + c2
+                        nc.vector.scalar_tensor_tensor(
+                            out=ep[:, c, :],
+                            in0=n_t[:, c, :],
+                            scalar=t_f[:, i0 + c : i0 + c + 1],
+                            in1=ep[:, c, :],
+                            op0=ALU.mult,
+                            op1=ALU.add,
                         )
-                        ncols = slice(1024 * h + 512 * nb, 1024 * h + 512 * (nb + 1))
-                        for mt in range(2):
-                            if g == 0:
-                                acc[(a, mt, nb)] = bank(4 * (1 - a) + 2 * mt + nb, [P, 512], "acc")
-                            nc.tensor.matmul_mx(
-                                out=acc[(a, mt, nb)][:],
-                                lhsT=stq[:, g, a, P * mt : P * (mt + 1)].bitcast(FP8X4),
-                                lhsT_scale=stqs[:, g, a, P * mt : P * (mt + 1)],
-                                rhs=cod[:].bitcast(FP8X4),
-                                rhs_scale=scl[:],
-                                start=(g == 0),
-                                stop=(g == 3),
-                            )
-                        if g == 3:
-                            for mt in range(2):
-                                if a == 1:
-                                    vt = work.tile([P, 512], F32, name="vt", bufs=2)
-                                    nc.vector.tensor_tensor(
-                                        out=vt[:], in0=acc[(a, mt, nb)][:], in1=s_sb[:, mt, ncols], op=ALU.mult
-                                    )
-                                    nc.vector.tensor_tensor(
-                                        out=nz[:, mt, ncols], in0=vt[:], in1=nz[:, mt, ncols], op=ALU.add
-                                    )
-                                else:
-                                    pre = work.tile([P, 512], F32, name="pre", bufs=2)
-                                    nc.vector.tensor_tensor(
-                                        out=pre[:], in0=acc[(a, mt, nb)][:], in1=nz[:, mt, ncols], op=ALU.add
-                                    )
-                                    o_t = work.tile([P, 512], F32, name="o_t")
-                                    nc.scalar.activation(out=o_t[:], in_=pre[:], func=ACT.Tanh)
-                                    nc.sync.dma_start(out=out[P * mt : P * (mt + 1), ncols], in_=o_t[:])
+                else:
+                    nc.vector.tensor_tensor(
+                        out=ep[:, pair, :], in0=acc[:], in1=ep[:, pair, :], op=ALU.add
+                    )
+            if a == 0:
+                for mt in range(2):
+                    ot = bank(mt, [P, 4, P], "ot")
+                    for c in range(4):
+                        nc.tensor.transpose(ot[:, c, :], ep[:, c, P * mt : P * (mt + 1)], ident[:])
+                    o_t = work.tile([P, 512], F32, name="o_t")
+                    nc.scalar.activation(
+                        out=o_t[:], in_=ot[:].rearrange("p c r -> p (c r)"), func=ACT.Tanh
+                    )
+                    nc.sync.dma_start(
+                        out=out[P * mt : P * (mt + 1), P * i0 : P * (i0 + 4)], in_=o_t[:]
+                    )
+
+        def regroup(engine_copy, grp, prod, c0, c1):
+            engine_copy(
+                out=grp[:, c0:c1, :].rearrange("p (c i) t -> p c t i", i=4),
+                in_=prod[:, :, c0:c1].rearrange("p t (c i) -> p c t i", i=4),
+            )
+
+        def unit(s, a, nb):
+            g = s % 4
+            src = sets[(s, "j" if a == 1 else "w")]
+            m_t = sets[(s, "m")]
+            c = slice(512 * nb, 512 * (nb + 1))
+            prod = work.tile([P, 4, 512], BF16, name="prod")
+            nc.vector.tensor_tensor(out=prod[:], in0=src[:, :, c], in1=m_t[:, :, c], op=ALU.mult)
+            grp = work.tile([P, 512, 4], BF16, name="grp", align_bytes=64)
+            split = 512 - (VECTOR_COLS if (a == 1 and nb == 0) else 0)
+            regroup(nc.scalar.copy, grp, prod, 0, split)
+            if split < 512:
+                regroup(nc.vector.tensor_copy, grp, prod, split, 512)
+            nc.vector.quantize_mx(
+                out=codes[:, a, g, nb, :].bitcast(FP8X4),
+                scales=scl[:, a, g, nb, :],
+                in_=grp[:].rearrange("p n t -> p (n t)"),
+            )
+
+        load_win(2)
+        stage_a(0)
+        load_win(3)
+        stage_b(0)
+        for s in range(2):
+            for kind in ("m", "j", "w"):
+                load_one(s, kind)
+        stage_a(1)
+        stage_c(0)
+        stage_b(1)
+        stage_a(2)
+        stage_c(1)
+        stage_b(2)
+        stage_a(3)
+        stage_c(2)
+        stage_b(3)
+        stage_c(3)
+
+        pending = []
+        count = 0
+        for s in range(8):
+            h = s // 4
+            for a in (1, 0):
+                for nb in range(2):
+                    unit(s, a, nb)
+                    for job in pending:
+                        finish(job[0], job[1], job[2])
+                    pending = []
+                    if s % 4 == 3:
+                        burst(h, a, nb)
+                        pending.append((h, a, nb))
+                    if count == 9:
+                        nc.sync.dma_start(
+                            out=noise[:], in_=noise_raw.rearrange("(t p) n -> p t n", p=P)
+                        )
+                    count += 1
+                if s + 2 < 8:
+                    if a == 1:
+                        load_one(s + 2, "j")
+                    else:
+                        load_one(s + 2, "m")
+                        load_one(s + 2, "w")
+        for job in pending:
+            finish(job[0], job[1], job[2])

@@ -20,7 +20,9 @@ FLOPS = 2 * M * DI * N + 2 * 2 * M * N * N
 PI_HI = 3.140625
 PI_LO = math.pi - PI_HI
 
-ACC_BANKS = (4, 5, 6, 2, 3)
+ACC_BANKS = (4, 5, 6, 2)
+NOISE_BANKS = (7, 3)
+LAGS = {(0, 1): (2, 2), (0, 0): (2, 2), (1, 1): (0, 2), (1, 0): (0, 0)}
 VECTOR_COLS = 256
 
 
@@ -212,7 +214,7 @@ def tile_brainquantumlayer_pa_kernel(
         def burst(h, a, nb):
             i0 = 8 * h + 4 * nb
             if a == 1:
-                n_t = bank(7, [P, 4, M], "n_t", BF16)
+                n_t = bank(NOISE_BANKS[nb], [P, 4, M], "n_t", BF16)
                 nts[(h, nb)] = n_t
                 for c in range(4):
                     for mt in range(2):
@@ -222,7 +224,7 @@ def tile_brainquantumlayer_pa_kernel(
                             ident_b[:],
                         )
             for q in range(2):
-                acc = bank(ACC_BANKS[acc_count[0] % 5], [P, 2, M], "acc")
+                acc = bank(ACC_BANKS[acc_count[0] % 4], [P, 2, M], "acc")
                 acc_count[0] += 1
                 accs[(h, a, nb, q)] = acc
                 for c2 in range(2):
@@ -325,29 +327,36 @@ def tile_brainquantumlayer_pa_kernel(
         stage_b(3)
         stage_c(3)
 
-        pending = []
+        jobs = {}
+
+        def later(index, job):
+            jobs[index] = jobs.get(index, []) + [job]
+
+        def run_jobs(index):
+            for job in jobs.get(index, []):
+                job[0](job[1], job[2], job[3])
+
         count = 0
         for s in range(8):
             h = s // 4
             for a in (1, 0):
                 for nb in range(2):
                     unit(s, a, nb)
-                    for job in pending:
-                        finish(job[0], job[1], job[2])
-                    pending = []
-                    if s % 4 == 3:
-                        burst(h, a, nb)
-                        pending.append((h, a, nb))
                     if count == 9:
                         nc.sync.dma_start(
                             out=noise[:], in_=noise_raw.rearrange("(t p) n -> p t n", p=P)
                         )
+                    if nb == 1 and s + 2 < 8:
+                        if a == 1:
+                            load_one(s + 2, "j")
+                        else:
+                            load_one(s + 2, "m")
+                            load_one(s + 2, "w")
+                    if s % 4 == 3:
+                        lag = LAGS[(h, a)]
+                        later(count + lag[0], (burst, h, a, nb))
+                        later(count + lag[0] + lag[1], (finish, h, a, nb))
+                    run_jobs(count)
                     count += 1
-                if s + 2 < 8:
-                    if a == 1:
-                        load_one(s + 2, "j")
-                    else:
-                        load_one(s + 2, "m")
-                        load_one(s + 2, "w")
-        for job in pending:
-            finish(job[0], job[1], job[2])
+        for index in range(count, count + 8):
+            run_jobs(index)

@@ -22,6 +22,8 @@ PI_LO = math.pi - PI_HI
 
 ACC_BANKS = (4, 5, 6, 2)
 NOISE_BANKS = (7, 3)
+TRANSPOSE_BANKS = (0, 1, 6)
+NOISE_AT = {0: 10, 1: 20}
 LAGS = {(0, 1): (2, 2), (0, 0): (2, 2), (1, 1): (0, 2), (1, 0): (0, 0)}
 VECTOR_COLS = 256
 
@@ -103,7 +105,7 @@ def tile_brainquantumlayer_pa_kernel(
         tr_count = [0]
 
         def transpose_words(src_f32, dst_f32):
-            ps = bank(tr_count[0] % 2, [P, 4, P], "tr_ps")
+            ps = bank(TRANSPOSE_BANKS[tr_count[0] % 3], [P, 4, P], "tr_ps")
             tr_count[0] += 1
             for q in range(4):
                 nc.tensor.transpose(ps[:, q, :], src_f32[:, P * q : P * (q + 1)], ident[:])
@@ -211,18 +213,19 @@ def tile_brainquantumlayer_pa_kernel(
 
         accs = {}
 
-        def burst(h, a, nb):
+        def transpose_noise(h, a, nb):
             i0 = 8 * h + 4 * nb
-            if a == 1:
-                n_t = bank(NOISE_BANKS[nb], [P, 4, M], "n_t", BF16)
-                nts[(h, nb)] = n_t
-                for c in range(4):
-                    for mt in range(2):
-                        nc.tensor.transpose(
-                            n_t[:, c, P * mt : P * (mt + 1)],
-                            noise[:, mt, P * (i0 + c) : P * (i0 + c + 1)],
-                            ident_b[:],
-                        )
+            n_t = bank(NOISE_BANKS[nb], [P, 4, M], "n_t", BF16)
+            nts[(h, nb)] = n_t
+            for c in range(4):
+                for mt in range(2):
+                    nc.tensor.transpose(
+                        n_t[:, c, P * mt : P * (mt + 1)],
+                        noise[:, mt, P * (i0 + c) : P * (i0 + c + 1)],
+                        ident_b[:],
+                    )
+
+        def burst(h, a, nb):
             for q in range(2):
                 acc = bank(ACC_BANKS[acc_count[0] % 4], [P, 2, M], "acc")
                 acc_count[0] += 1
@@ -277,7 +280,7 @@ def tile_brainquantumlayer_pa_kernel(
                     ot = bank(mt, [P, 4, P], "ot")
                     for c in range(4):
                         nc.tensor.transpose(ot[:, c, :], ep[:, c, P * mt : P * (mt + 1)], ident[:])
-                    o_t = work.tile([P, 512], F32, name="o_t")
+                    o_t = work.tile([P, 512], F32, name="o_t", bufs=4)
                     nc.scalar.activation(
                         out=o_t[:], in_=ot[:].rearrange("p c r -> p (c r)"), func=ACT.Tanh
                     )
@@ -335,6 +338,10 @@ def tile_brainquantumlayer_pa_kernel(
         def run_jobs(index):
             for job in jobs.get(index, []):
                 job[0](job[1], job[2], job[3])
+
+        for h in range(2):
+            for nb in range(2):
+                later(NOISE_AT[h] + nb, (transpose_noise, h, 1, nb))
 
         count = 0
         for s in range(8):

@@ -20,11 +20,21 @@ FLOPS = 2 * M * DI * N + 2 * 2 * M * N * N
 PI_HI = 3.140625
 PI_LO = math.pi - PI_HI
 
-ACC_BANKS = (4, 5, 6, 2)
+GROUP_BANKS = {
+    (0, 1, 0): (4, 5),
+    (0, 1, 1): (6, 2),
+    (0, 0, 0): (4, 5),
+    (0, 0, 1): (6, 2),
+    (1, 1, 0): (0, 1),
+    (1, 1, 1): (7, 3),
+    (1, 0, 0): (4, 5),
+    (1, 0, 1): (6, 2),
+}
 NOISE_BANKS = (7, 3)
 TRANSPOSE_BANKS = (0, 1, 6)
 NOISE_AT = {0: 10, 1: 20}
-LAGS = {(0, 1): (2, 2), (0, 0): (2, 2), (1, 1): (0, 2), (1, 0): (0, 0)}
+LAGS = {(0, 1): 4, (0, 0): 4, (1, 1): 2, (1, 0): 0}
+OPEN_LAG = 2
 VECTOR_COLS = 256
 
 
@@ -197,7 +207,6 @@ def tile_brainquantumlayer_pa_kernel(
         sets = {}
         eps = {}
         nts = {}
-        acc_count = [0]
 
         def load_one(s, kind):
             h, g = divmod(s, 4)
@@ -224,24 +233,43 @@ def tile_brainquantumlayer_pa_kernel(
                         noise[:, mt, P * (i0 + c) : P * (i0 + c + 1)],
                         ident_b[:],
                     )
+            if h == 1:
+                n_sb = work.tile([P, 4, M], BF16, name="n_sb", bufs=2)
+                nc.scalar.copy(out=n_sb[:], in_=n_t[:])
+                nts[(h, nb)] = n_sb
+                if nb == 1:
+                    open_group(1, 1, 1)
 
-        def burst(h, a, nb):
+        waiting = {}
+
+        def passes(h, a, nb, g):
             for q in range(2):
-                acc = bank(ACC_BANKS[acc_count[0] % 4], [P, 2, M], "acc")
-                acc_count[0] += 1
-                accs[(h, a, nb, q)] = acc
+                acc = accs[(h, a, nb)][q]
                 for c2 in range(2):
                     c = 2 * q + c2
-                    for gg in range(4):
-                        nc.tensor.matmul_mx(
-                            out=acc[:, c2, :],
-                            lhsT=codes[:, a, gg, nb, P * c : P * (c + 1)].bitcast(FP8X4),
-                            lhsT_scale=scl[:, a, gg, nb, P * c : P * (c + 1)],
-                            rhs=stq[:, gg, a, :].bitcast(FP8X4),
-                            rhs_scale=stqs[:, gg, a, :],
-                            start=(gg == 0),
-                            stop=(gg == 3),
-                        )
+                    nc.tensor.matmul_mx(
+                        out=acc[:, c2, :],
+                        lhsT=codes[:, a, g, nb, P * c : P * (c + 1)].bitcast(FP8X4),
+                        lhsT_scale=scl[:, a, g, nb, P * c : P * (c + 1)],
+                        rhs=stq[:, g, a, :].bitcast(FP8X4),
+                        rhs_scale=stqs[:, g, a, :],
+                        start=(g == 0 and c2 == 0),
+                        stop=(g == 3 and c2 == 1),
+                    )
+
+        def open_group(h, a, nb):
+            banks = GROUP_BANKS[(h, a, nb)]
+            acc0 = bank(banks[0], [P, 2, M], "acc")
+            acc1 = bank(banks[1], [P, 2, M], "acc")
+            accs[(h, a, nb)] = (acc0, acc1)
+            for g in waiting.get((h, a, nb), []):
+                passes(h, a, nb, g)
+
+        def codes_ready(h, a, nb, g):
+            if (h, a, nb) in accs:
+                passes(h, a, nb, g)
+            else:
+                waiting[(h, a, nb)] = waiting.get((h, a, nb), []) + [g]
 
         def finish(h, a, nb):
             i0 = 8 * h + 4 * nb
@@ -250,7 +278,7 @@ def tile_brainquantumlayer_pa_kernel(
             ep = eps[(h, nb)]
             n_t = nts[(h, nb)]
             for q in range(2):
-                acc = accs[(h, a, nb, q)]
+                acc = accs[(h, a, nb)][q]
                 pair = slice(2 * q, 2 * q + 2)
                 if a == 1:
                     nc.vector.scalar_tensor_tensor(
@@ -287,6 +315,10 @@ def tile_brainquantumlayer_pa_kernel(
                     nc.sync.dma_start(
                         out=out[P * mt : P * (mt + 1), P * i0 : P * (i0 + 4)], in_=o_t[:]
                     )
+            if a == 0 and h == 0:
+                open_group(1, 0, nb)
+                if nb == 1:
+                    open_group(1, 1, 0)
 
         def regroup(engine_copy, grp, prod, c0, c1):
             engine_copy(
@@ -311,6 +343,7 @@ def tile_brainquantumlayer_pa_kernel(
                 scales=scl[:, a, g, nb, :],
                 in_=grp[:].rearrange("p n t -> p (n t)"),
             )
+            codes_ready(s // 4, a, nb, g)
 
         load_win(2)
         stage_a(0)
@@ -360,9 +393,9 @@ def tile_brainquantumlayer_pa_kernel(
                             load_one(s + 2, "m")
                             load_one(s + 2, "w")
                     if s % 4 == 3:
-                        lag = LAGS[(h, a)]
-                        later(count + lag[0], (burst, h, a, nb))
-                        later(count + lag[0] + lag[1], (finish, h, a, nb))
+                        if h == 0:
+                            later(count + OPEN_LAG, (open_group, h, a, nb))
+                        later(count + LAGS[(h, a)], (finish, h, a, nb))
                     run_jobs(count)
                     count += 1
         for index in range(count, count + 8):

@@ -19,6 +19,7 @@ FLOPS = 2 * M * DI * N + 2 * 2 * M * N * N
 
 PI_HI = 3.140625
 PI_LO = math.pi - PI_HI
+TAYLOR = [(-1.0) ** k / math.factorial(2 * k + 1) for k in range(9)]
 
 GROUP_BANKS = {
     (0, 1, 0): (4, 5),
@@ -52,8 +53,30 @@ def tile_brainquantumlayer_pa_kernel(
         def bank(i, shape, name, dtype=F32):
             return psum.tile(shape, dtype, tag="bank%d" % i, name=name)
 
+        sets = {}
+
+        def load_cols(s, kind, c0, c1):
+            h, g = divmod(s, 4)
+            src = {"m": mask, "j": J, "w": weights}[kind]
+            if c0 == 0:
+                t_in = stream.tile([P, 4, 1024], BF16, name="in_" + kind, tag="in_" + kind)
+                sets[(s, kind)] = t_in
+            nc.sync.dma_start(
+                out=sets[(s, kind)][:, :, c0:c1],
+                in_=src[512 * g : 512 * (g + 1), 1024 * h + c0 : 1024 * h + c1].rearrange(
+                    "(t p) n -> p t n", p=P
+                ),
+            )
+
+        def load_one(s, kind):
+            load_cols(s, kind, 0, 1024)
+
+        load_cols(0, "m", 0, 256)
+        load_cols(0, "j", 0, 256)
         x_sb = early.tile([P, 2, DI], BF16, name="x_sb", tag="win", bufs=3)
         nc.sync.dma_start(out=x_sb[:], in_=x.rearrange("(t p) k -> p t k", p=P))
+        load_cols(0, "m", 256, 512)
+        load_cols(0, "j", 256, 512)
         wins = {}
 
         def load_win(g):
@@ -64,8 +87,13 @@ def tile_brainquantumlayer_pa_kernel(
             wins[g] = win
 
         load_win(0)
-        load_win(1)
+        load_cols(0, "m", 512, 1024)
+        load_cols(0, "j", 512, 1024)
 
+        dummy = const.tile([P, 1], F32, name="dummy")
+        nc.vector.memset(dummy[:], 0.0)
+        warm = const.tile([P, 1], F32, name="warm")
+        nc.scalar.activation(out=warm[:], in_=dummy[:], func=ACT.Tanh)
         ident = const.tile([P, P], F32, name="ident")
         make_identity(nc, ident[:])
         ident_b = const.tile([P, P], BF16, name="ident_b")
@@ -101,14 +129,28 @@ def tile_brainquantumlayer_pa_kernel(
         nc.vector.scalar_tensor_tensor(
             out=r2[:], in0=nf[:], scalar=-PI_LO, in1=r1[:], op0=ALU.mult, op1=ALU.add
         )
-        sn = const.tile([P, 16], F32, name="sn")
-        nc.scalar.activation(out=sn[:], in_=r2[:], func=ACT.Sin)
-        s01 = const.tile([P, 16], F32, name="s01")
-        nc.vector.tensor_scalar_mul(out=s01[:], in0=sn[:], scalar1=0.1)
-        t_f = const.tile([P, 16], F32, name="t_f")
-        nc.vector.scalar_tensor_tensor(
-            out=t_f[:], in0=s01[:], scalar=-1.0, in1=s01[:], op0=ALU.mult, op1=ALU.max
+        sq = const.tile([P, 16], F32, name="sq")
+        nc.gpsimd.tensor_tensor(out=sq[:], in0=r2[:], in1=r2[:], op=ALU.mult)
+        poly = const.tile([P, 16], F32, name="poly")
+        nc.gpsimd.tensor_scalar(
+            out=poly[:], in0=sq[:], scalar1=TAYLOR[8], scalar2=TAYLOR[7], op0=ALU.mult, op1=ALU.add
         )
+        for k in range(6, -1, -1):
+            nc.gpsimd.tensor_tensor(out=poly[:], in0=poly[:], in1=sq[:], op=ALU.mult)
+            nc.gpsimd.tensor_scalar(
+                out=poly[:], in0=poly[:], scalar1=1.0, scalar2=TAYLOR[k], op0=ALU.mult, op1=ALU.add
+            )
+        nc.gpsimd.tensor_tensor(out=poly[:], in0=poly[:], in1=r2[:], op=ALU.mult)
+        s01 = const.tile([P, 16], F32, name="s01")
+        nc.gpsimd.tensor_scalar(
+            out=s01[:], in0=poly[:], scalar1=0.1, scalar2=0.0, op0=ALU.mult, op1=ALU.add
+        )
+        t_f = const.tile([P, 16], F32, name="t_f")
+
+        def finish_t():
+            nc.vector.scalar_tensor_tensor(
+                out=t_f[:], in0=s01[:], scalar=-1.0, in1=s01[:], op0=ALU.mult, op1=ALU.max
+            )
         lam_f = const.tile([P, 1], F32, name="lam_f")
         nc.vector.tensor_copy(out=lam_f[:], in_=lam_b[:])
 
@@ -122,19 +164,21 @@ def tile_brainquantumlayer_pa_kernel(
             view = ps[:].rearrange("p (c u) r -> p c r u", u=2)
             nc.scalar.copy(out=dst_f32, in_=view)
 
-        xg = early.tile([P, 2, 2 * P, 4], BF16, name="xg", tag="wgrp", align_bytes=64)
-        for t in range(2):
-            transpose_words(
-                x_sb[:].bitcast(F32)[:, t, :],
-                xg[:].bitcast(F32)[:, :, P * t : P * (t + 1), :],
-            )
         xq = const.tile([P, 2, 2 * P], U32, name="xq", align_bytes=64)
         xqs = const.tile([P, 2, 2 * P], U8, name="xqs", align_bytes=64)
-        nc.vector.quantize_mx(
-            out=xq[:].rearrange("p c w -> p (c w)").bitcast(FP8X4),
-            scales=xqs[:].rearrange("p c w -> p (c w)"),
-            in_=xg[:].rearrange("p c w t -> p (c w t)"),
-        )
+
+        def stage_x():
+            xg = early.tile([P, 2, 2 * P, 4], BF16, name="xg", tag="wgrp", align_bytes=64)
+            for t in range(2):
+                transpose_words(
+                    x_sb[:].bitcast(F32)[:, t, :],
+                    xg[:].bitcast(F32)[:, :, P * t : P * (t + 1), :],
+                )
+            nc.vector.quantize_mx(
+                out=xq[:].rearrange("p c w -> p (c w)").bitcast(FP8X4),
+                scales=xqs[:].rearrange("p c w -> p (c w)"),
+                in_=xg[:].rearrange("p c w t -> p (c w t)"),
+            )
 
         stq = const.tile([P, 4, 2, M], U32, name="stq", align_bytes=64)
         stqs = const.tile([P, 4, 2, M], U8, name="stqs", align_bytes=64)
@@ -204,21 +248,8 @@ def tile_brainquantumlayer_pa_kernel(
         codes = const.tile([P, 2, 4, 2, 512], U32, name="codes", align_bytes=64)
         scl = const.tile([P, 2, 4, 2, 512], U8, name="scl", align_bytes=64)
         noise = const.tile([P, 2, N], BF16, name="noise")
-        sets = {}
         eps = {}
         nts = {}
-
-        def load_one(s, kind):
-            h, g = divmod(s, 4)
-            src = {"m": mask, "j": J, "w": weights}[kind]
-            t_in = stream.tile([P, 4, 1024], BF16, name="in_" + kind, tag="in_" + kind)
-            nc.sync.dma_start(
-                out=t_in[:],
-                in_=src[512 * g : 512 * (g + 1), 1024 * h : 1024 * (h + 1)].rearrange(
-                    "(t p) n -> p t n", p=P
-                ),
-            )
-            sets[(s, kind)] = t_in
 
         accs = {}
 
@@ -330,9 +361,13 @@ def tile_brainquantumlayer_pa_kernel(
             g = s % 4
             src = sets[(s, "j" if a == 1 else "w")]
             m_t = sets[(s, "m")]
-            c = slice(512 * nb, 512 * (nb + 1))
             prod = work.tile([P, 4, 512], BF16, name="prod")
-            nc.vector.tensor_tensor(out=prod[:], in0=src[:, :, c], in1=m_t[:, :, c], op=ALU.mult)
+            pieces = [(0, 256), (256, 512)] if (s == 0 and a == 1 and nb == 0) else [(0, 512)]
+            for c0, c1 in pieces:
+                c = slice(512 * nb + c0, 512 * nb + c1)
+                nc.vector.tensor_tensor(
+                    out=prod[:, :, c0:c1], in0=src[:, :, c], in1=m_t[:, :, c], op=ALU.mult
+                )
             grp = work.tile([P, 512, 4], BF16, name="grp", align_bytes=64)
             split = 512 - (VECTOR_COLS if (a == 1 and nb == 0) else 0)
             regroup(nc.scalar.copy, grp, prod, 0, split)
@@ -345,24 +380,25 @@ def tile_brainquantumlayer_pa_kernel(
             )
             codes_ready(s // 4, a, nb, g)
 
+        load_one(0, "w")
+        load_win(1)
+        load_one(1, "m")
+        load_one(1, "j")
         load_win(2)
-        stage_a(0)
+        load_one(1, "w")
         load_win(3)
-        stage_b(0)
-        for s in range(2):
-            for kind in ("m", "j", "w"):
-                load_one(s, kind)
-        stage_a(1)
-        stage_c(0)
-        stage_b(1)
-        stage_a(2)
-        stage_c(1)
-        stage_b(2)
-        stage_a(3)
-        stage_c(2)
-        stage_b(3)
-        stage_c(3)
 
+        first_stage = {
+            1: [stage_x, lambda: stage_a(0)],
+            2: [lambda: stage_b(0)],
+            3: [lambda: stage_a(1), lambda: stage_c(0)],
+            4: [lambda: stage_b(1)],
+            5: [lambda: stage_a(2), lambda: stage_c(1)],
+            6: [lambda: stage_b(2)],
+            7: [lambda: stage_a(3), lambda: stage_c(2)],
+            8: [lambda: stage_b(3)],
+            9: [lambda: stage_c(3), finish_t],
+        }
         jobs = {}
 
         def later(index, job):
@@ -381,6 +417,8 @@ def tile_brainquantumlayer_pa_kernel(
             h = s // 4
             for a in (1, 0):
                 for nb in range(2):
+                    for job in first_stage.get(count, []):
+                        job()
                     unit(s, a, nb)
                     if count == 9:
                         nc.sync.dma_start(

@@ -36,7 +36,11 @@ TRANSPOSE_BANKS = (0, 1, 6)
 NOISE_AT = {0: 10, 1: 20}
 LAGS = {(0, 1): 4, (0, 0): 4, (1, 1): 2, (1, 0): 0}
 OPEN_LAG = 2
-VECTOR_COLS = 256
+FINE = {
+    0: (((0, 256), (256, 512)), ((512, 1024),)),
+    28: (((0, 512),), ((512, 1024),)),
+    30: (((0, 512),), ((512, 1024),)),
+}
 
 
 def tile_brainquantumlayer_pa_kernel(
@@ -247,7 +251,7 @@ def tile_brainquantumlayer_pa_kernel(
 
         codes = const.tile([P, 2, 4, 2, 512], U32, name="codes", align_bytes=64)
         scl = const.tile([P, 2, 4, 2, 512], U8, name="scl", align_bytes=64)
-        noise = const.tile([P, 2, N], BF16, name="noise")
+        noise = early.tile([P, 2, N], BF16, name="noise", tag="win", bufs=3)
         eps = {}
         nts = {}
 
@@ -305,7 +309,7 @@ def tile_brainquantumlayer_pa_kernel(
         def finish(h, a, nb):
             i0 = 8 * h + 4 * nb
             if a == 1:
-                eps[(h, nb)] = work.tile([P, 4, M], F32, name="ep", bufs=2)
+                eps[(h, nb)] = early.tile([P, 4, M], F32, name="ep", tag="wgrp", align_bytes=64)
             ep = eps[(h, nb)]
             n_t = nts[(h, nb)]
             for q in range(2):
@@ -339,7 +343,7 @@ def tile_brainquantumlayer_pa_kernel(
                     ot = bank(mt, [P, 4, P], "ot")
                     for c in range(4):
                         nc.tensor.transpose(ot[:, c, :], ep[:, c, P * mt : P * (mt + 1)], ident[:])
-                    o_t = work.tile([P, 512], F32, name="o_t", bufs=4)
+                    o_t = early.tile([P, 512], F32, name="o_t", tag="gst", align_bytes=64)
                     nc.scalar.activation(
                         out=o_t[:], in_=ot[:].rearrange("p c r -> p (c r)"), func=ACT.Tanh
                     )
@@ -357,28 +361,28 @@ def tile_brainquantumlayer_pa_kernel(
                 in_=prod[:, :, c0:c1].rearrange("p t (c i) -> p c t i", i=4),
             )
 
-        def unit(s, a, nb):
+        def unit(s, a, c0, c1):
             g = s % 4
+            width = c1 - c0
             src = sets[(s, "j" if a == 1 else "w")]
             m_t = sets[(s, "m")]
-            prod = work.tile([P, 4, 512], BF16, name="prod")
-            pieces = [(0, 256), (256, 512)] if (s == 0 and a == 1 and nb == 0) else [(0, 512)]
-            for c0, c1 in pieces:
-                c = slice(512 * nb + c0, 512 * nb + c1)
-                nc.vector.tensor_tensor(
-                    out=prod[:, :, c0:c1], in0=src[:, :, c], in1=m_t[:, :, c], op=ALU.mult
-                )
-            grp = work.tile([P, 512, 4], BF16, name="grp", align_bytes=64)
-            split = 512 - (VECTOR_COLS if (a == 1 and nb == 0) else 0)
-            regroup(nc.scalar.copy, grp, prod, 0, split)
-            if split < 512:
-                regroup(nc.vector.tensor_copy, grp, prod, split, 512)
-            nc.vector.quantize_mx(
-                out=codes[:, a, g, nb, :].bitcast(FP8X4),
-                scales=scl[:, a, g, nb, :],
-                in_=grp[:].rearrange("p n t -> p (n t)"),
+            prod = work.tile([P, 4, 1024], BF16, name="prod")
+            nc.vector.tensor_tensor(
+                out=prod[:, :, :width], in0=src[:, :, c0:c1], in1=m_t[:, :, c0:c1], op=ALU.mult
             )
-            codes_ready(s // 4, a, nb, g)
+            grp = work.tile([P, 1024, 4], BF16, name="grp", align_bytes=64)
+            split = width - (width // 4 if a == 1 else 0)
+            regroup(nc.scalar.copy, grp, prod, 0, split)
+            if split < width:
+                regroup(nc.vector.tensor_copy, grp, prod, split, width)
+            nc.vector.quantize_mx(
+                out=codes[:, a, g].rearrange("p b n -> p (b n)")[:, c0:c1].bitcast(FP8X4),
+                scales=scl[:, a, g].rearrange("p b n -> p (b n)")[:, c0:c1],
+                in_=grp[:, :width, :].rearrange("p n t -> p (n t)"),
+            )
+            for nb in range(2):
+                if c0 < 512 * (nb + 1) <= c1:
+                    codes_ready(s // 4, a, nb, g)
 
         load_one(0, "w")
         load_win(1)
@@ -416,14 +420,19 @@ def tile_brainquantumlayer_pa_kernel(
         for s in range(8):
             h = s // 4
             for a in (1, 0):
+                fine = FINE.get(count)
                 for nb in range(2):
                     for job in first_stage.get(count, []):
                         job()
-                    unit(s, a, nb)
                     if count == 9:
                         nc.sync.dma_start(
                             out=noise[:], in_=noise_raw.rearrange("(t p) n -> p t n", p=P)
                         )
+                    if fine:
+                        for c0, c1 in fine[nb]:
+                            unit(s, a, c0, c1)
+                    elif nb == 0:
+                        unit(s, a, 0, 1024)
                     if nb == 1 and s + 2 < 8:
                         if a == 1:
                             load_one(s + 2, "j")

@@ -21,26 +21,17 @@ PI_HI = 3.140625
 PI_LO = math.pi - PI_HI
 TAYLOR = [(-1.0) ** k / math.factorial(2 * k + 1) for k in range(9)]
 
-GROUP_BANKS = {
-    (0, 1, 0): (4, 5),
-    (0, 1, 1): (6, 2),
-    (0, 0, 0): (4, 5),
-    (0, 0, 1): (6, 2),
-    (1, 1, 0): (0, 1),
-    (1, 1, 1): (7, 3),
-    (1, 0, 0): (4, 5),
-    (1, 0, 1): (6, 2),
-}
+
+UNITS = [(0, 1, 0, 256), (0, 1, 256, 512), (0, 1, 512, 1024), (0, 0, 0, 512), (0, 0, 512, 1024)]
+UNITS = UNITS + [(s, a, 0, 1024) for s in range(1, 5) for a in (1, 0)]
+UNITS = UNITS + [(5, 1, 0, 1024), (6, 1, 0, 1024), (7, 1, 0, 1024), (5, 0, 0, 1024), (6, 0, 0, 1024)]
+UNITS = UNITS + [(7, 0, 0, 512), (7, 0, 512, 768), (7, 0, 768, 1024)]
+LAST_PRODUCT = len(UNITS) - 3
+VECTOR_COLS = {5: 512, 6: 512, 7: 512, 8: 512, 9: 256}
+PAIR_BANKS = {(0, 1): (4, 5, 6, 2), (0, 0): (0, 1, 4, 5), (1, 1): (4, 5, 6, 2), (1, 0): (0, 1, 7, 3)}
 NOISE_BANKS = (7, 3)
-TRANSPOSE_BANKS = (0, 1, 6)
-NOISE_AT = {0: 10, 1: 20}
-LAGS = {(0, 1): 4, (0, 0): 4, (1, 1): 2, (1, 0): 0}
-OPEN_LAG = 2
-FINE = {
-    0: (((0, 256), (256, 512)), ((512, 1024),)),
-    28: (((0, 512),), ((512, 1024),)),
-    30: (((0, 512),), ((512, 1024),)),
-}
+TRANSPOSE_BANKS = (0, 1, 6, 7)
+OUT_BANKS = {0: (6, 2, 6, 2), 1: (4, 5, 6, 2)}
 
 
 def tile_brainquantumlayer_pa_kernel(
@@ -53,6 +44,11 @@ def tile_brainquantumlayer_pa_kernel(
         stream = ctx.enter_context(tc.tile_pool(name="stream", bufs=2))
         work = ctx.enter_context(tc.tile_pool(name="work", bufs=3))
         psum = ctx.enter_context(tc.psum_pool(name="psum", bufs=1))
+        ctx.enter_context(
+            tc.manual_schedule(
+                engines={mybir.EngineType.PE, mybir.EngineType.Activation, mybir.EngineType.DVE}
+            )
+        )
 
         def bank(i, shape, name, dtype=F32):
             return psum.tile(shape, dtype, tag="bank%d" % i, name=name)
@@ -63,7 +59,9 @@ def tile_brainquantumlayer_pa_kernel(
             h, g = divmod(s, 4)
             src = {"m": mask, "j": J, "w": weights}[kind]
             if c0 == 0:
-                t_in = stream.tile([P, 4, 1024], BF16, name="in_" + kind, tag="in_" + kind)
+                t_in = stream.tile(
+                    [P, 4, 1024], BF16, name="in_" + kind, tag="in_" + kind, bufs=3 if kind == "m" else 2
+                )
                 sets[(s, kind)] = t_in
             nc.sync.dma_start(
                 out=sets[(s, kind)][:, :, c0:c1],
@@ -72,8 +70,14 @@ def tile_brainquantumlayer_pa_kernel(
                 ),
             )
 
-        def load_one(s, kind):
-            load_cols(s, kind, 0, 1024)
+        wins = {}
+
+        def load_win(g):
+            win = early.tile([P, 4, DI], BF16, name="win", tag="win", bufs=3)
+            nc.sync.dma_start(
+                out=win[:], in_=W_in[512 * g : 512 * (g + 1), :].rearrange("(t p) k -> p t k", p=P)
+            )
+            wins[g] = win
 
         load_cols(0, "m", 0, 256)
         load_cols(0, "j", 0, 256)
@@ -81,18 +85,17 @@ def tile_brainquantumlayer_pa_kernel(
         nc.sync.dma_start(out=x_sb[:], in_=x.rearrange("(t p) k -> p t k", p=P))
         load_cols(0, "m", 256, 512)
         load_cols(0, "j", 256, 512)
-        wins = {}
-
-        def load_win(g):
-            win = early.tile([P, 4, DI], BF16, name="win", tag="win", bufs=3)
-            for t in range(4):
-                r0 = 512 * g + P * t
-                nc.sync.dma_start(out=win[:, t, :], in_=W_in[r0 : r0 + P, :])
-            wins[g] = win
-
-        load_win(0)
         load_cols(0, "m", 512, 1024)
         load_cols(0, "j", 512, 1024)
+        load_win(0)
+        load_cols(0, "w", 0, 1024)
+        load_win(1)
+        load_cols(1, "m", 0, 1024)
+        load_cols(1, "j", 0, 1024)
+        load_win(2)
+        load_cols(1, "w", 0, 1024)
+        load_win(3)
+        load_cols(2, "m", 0, 1024)
 
         dummy = const.tile([P, 1], F32, name="dummy")
         nc.vector.memset(dummy[:], 0.0)
@@ -109,75 +112,83 @@ def tile_brainquantumlayer_pa_kernel(
         nc.scalar.dma_start(out=vecs[16:32, :], in_=theta.rearrange("(i p) -> i p", p=P))
         lam_b = const.tile([P, 1], BF16, name="lam_b")
         nc.scalar.dma_start(out=lam_b[:], in_=lam.partition_broadcast(P))
-
-        vps = bank(0, [P, P], "vps", BF16)
-        nc.tensor.transpose(vps[:], vecs[:], ident_b[:])
         vec_f = const.tile([P, 32], F32, name="vec_f")
-        nc.vector.tensor_copy(out=vec_f[:], in_=vps[:, 0:32])
         bias_f = vec_f[:, 0:16]
-        th_f = vec_f[:, 16:32]
-
-        tq = const.tile([P, 16], F32, name="tq")
-        nc.vector.tensor_scalar_mul(out=tq[:], in0=th_f, scalar1=2.0 / math.pi)
-        ni = const.tile([P, 16], I32, name="ni")
-        nc.vector.tensor_copy(out=ni[:], in_=tq[:])
-        nf = const.tile([P, 16], F32, name="nf")
-        nc.vector.tensor_copy(out=nf[:], in_=ni[:])
-        y2 = const.tile([P, 16], F32, name="y2")
-        nc.vector.tensor_scalar_mul(out=y2[:], in0=th_f, scalar1=2.0)
-        r1 = const.tile([P, 16], F32, name="r1")
-        nc.vector.scalar_tensor_tensor(
-            out=r1[:], in0=nf[:], scalar=-PI_HI, in1=y2[:], op0=ALU.mult, op1=ALU.add
-        )
-        r2 = const.tile([P, 16], F32, name="r2")
-        nc.vector.scalar_tensor_tensor(
-            out=r2[:], in0=nf[:], scalar=-PI_LO, in1=r1[:], op0=ALU.mult, op1=ALU.add
-        )
-        sq = const.tile([P, 16], F32, name="sq")
-        nc.gpsimd.tensor_tensor(out=sq[:], in0=r2[:], in1=r2[:], op=ALU.mult)
-        poly = const.tile([P, 16], F32, name="poly")
-        nc.gpsimd.tensor_scalar(
-            out=poly[:], in0=sq[:], scalar1=TAYLOR[8], scalar2=TAYLOR[7], op0=ALU.mult, op1=ALU.add
-        )
-        for k in range(6, -1, -1):
-            nc.gpsimd.tensor_tensor(out=poly[:], in0=poly[:], in1=sq[:], op=ALU.mult)
-            nc.gpsimd.tensor_scalar(
-                out=poly[:], in0=poly[:], scalar1=1.0, scalar2=TAYLOR[k], op0=ALU.mult, op1=ALU.add
-            )
-        nc.gpsimd.tensor_tensor(out=poly[:], in0=poly[:], in1=r2[:], op=ALU.mult)
+        lam_f = const.tile([P, 1], F32, name="lam_f")
         s01 = const.tile([P, 16], F32, name="s01")
-        nc.gpsimd.tensor_scalar(
-            out=s01[:], in0=poly[:], scalar1=0.1, scalar2=0.0, op0=ALU.mult, op1=ALU.add
-        )
         t_f = const.tile([P, 16], F32, name="t_f")
+
+        def small_vectors():
+            vps = bank(2, [P, P], "vps", BF16)
+            nc.tensor.transpose(vps[:], vecs[:], ident_b[:])
+            nc.vector.tensor_copy(out=vec_f[:], in_=vps[:, 0:32])
+            nc.vector.tensor_copy(out=lam_f[:], in_=lam_b[:])
+            th_f = vec_f[:, 16:32]
+            tq = const.tile([P, 16], F32, name="tq")
+            nc.vector.tensor_scalar_mul(out=tq[:], in0=th_f, scalar1=2.0 / math.pi)
+            ni = const.tile([P, 16], I32, name="ni")
+            nc.vector.tensor_copy(out=ni[:], in_=tq[:])
+            nf = const.tile([P, 16], F32, name="nf")
+            nc.vector.tensor_copy(out=nf[:], in_=ni[:])
+            y2 = const.tile([P, 16], F32, name="y2")
+            nc.vector.tensor_scalar_mul(out=y2[:], in0=th_f, scalar1=2.0)
+            r1 = const.tile([P, 16], F32, name="r1")
+            nc.vector.scalar_tensor_tensor(
+                out=r1[:], in0=nf[:], scalar=-PI_HI, in1=y2[:], op0=ALU.mult, op1=ALU.add
+            )
+            r2 = const.tile([P, 16], F32, name="r2")
+            nc.vector.scalar_tensor_tensor(
+                out=r2[:], in0=nf[:], scalar=-PI_LO, in1=r1[:], op0=ALU.mult, op1=ALU.add
+            )
+            sq = const.tile([P, 16], F32, name="sq")
+            nc.gpsimd.tensor_tensor(out=sq[:], in0=r2[:], in1=r2[:], op=ALU.mult)
+            poly = const.tile([P, 16], F32, name="poly")
+            nc.gpsimd.tensor_scalar(
+                out=poly[:], in0=sq[:], scalar1=TAYLOR[8], scalar2=TAYLOR[7], op0=ALU.mult, op1=ALU.add
+            )
+            for k in range(6, -1, -1):
+                nc.gpsimd.tensor_tensor(out=poly[:], in0=poly[:], in1=sq[:], op=ALU.mult)
+                nc.gpsimd.tensor_scalar(
+                    out=poly[:], in0=poly[:], scalar1=1.0, scalar2=TAYLOR[k], op0=ALU.mult, op1=ALU.add
+                )
+            nc.gpsimd.tensor_tensor(out=poly[:], in0=poly[:], in1=r2[:], op=ALU.mult)
+            nc.gpsimd.tensor_scalar(
+                out=s01[:], in0=poly[:], scalar1=0.1, scalar2=0.0, op0=ALU.mult, op1=ALU.add
+            )
 
         def finish_t():
             nc.vector.scalar_tensor_tensor(
                 out=t_f[:], in0=s01[:], scalar=-1.0, in1=s01[:], op0=ALU.mult, op1=ALU.max
             )
-        lam_f = const.tile([P, 1], F32, name="lam_f")
-        nc.vector.tensor_copy(out=lam_f[:], in_=lam_b[:])
 
         tr_count = [0]
+        tr_ps = {}
 
-        def transpose_words(src_f32, dst_f32):
-            ps = bank(TRANSPOSE_BANKS[tr_count[0] % 3], [P, 4, P], "tr_ps")
+        def transpose_words(key, src_f32):
+            i = TRANSPOSE_BANKS[tr_count[0] % len(TRANSPOSE_BANKS)]
+            ps = bank(i, [P, 4, P], "tr_ps")
             tr_count[0] += 1
+            tr_ps[key] = ps
             for q in range(4):
                 nc.tensor.transpose(ps[:, q, :], src_f32[:, P * q : P * (q + 1)], ident[:])
-            view = ps[:].rearrange("p (c u) r -> p c r u", u=2)
+
+        def copy_words(key, dst_f32):
+            view = tr_ps[key][:].rearrange("p (c u) r -> p c r u", u=2)
             nc.scalar.copy(out=dst_f32, in_=view)
 
+        xg = early.tile([P, 2, 2 * P, 4], BF16, name="xg", tag="wgrp", align_bytes=64)
         xq = const.tile([P, 2, 2 * P], U32, name="xq", align_bytes=64)
         xqs = const.tile([P, 2, 2 * P], U8, name="xqs", align_bytes=64)
 
-        def stage_x():
-            xg = early.tile([P, 2, 2 * P, 4], BF16, name="xg", tag="wgrp", align_bytes=64)
+        def x_transposes():
             for t in range(2):
-                transpose_words(
-                    x_sb[:].bitcast(F32)[:, t, :],
-                    xg[:].bitcast(F32)[:, :, P * t : P * (t + 1), :],
-                )
+                transpose_words(("x", t), x_sb[:].bitcast(F32)[:, t, :])
+
+        def x_copies():
+            for t in range(2):
+                copy_words(("x", t), xg[:].bitcast(F32)[:, :, P * t : P * (t + 1), :])
+
+        def x_codes():
             nc.vector.quantize_mx(
                 out=xq[:].rearrange("p c w -> p (c w)").bitcast(FP8X4),
                 scales=xqs[:].rearrange("p c w -> p (c w)"),
@@ -187,263 +198,304 @@ def tile_brainquantumlayer_pa_kernel(
         stq = const.tile([P, 4, 2, M], U32, name="stq", align_bytes=64)
         stqs = const.tile([P, 4, 2, M], U8, name="stqs", align_bytes=64)
         sT = const.tile([P, 16, M], F32, name="sT")
-
         wgrps = {}
+        wqs = {}
+        sts = {}
         stbs = {}
 
-        def stage_a(g):
-            win = wins[g]
+        def win_transposes(g):
+            for t in range(4):
+                transpose_words((g, t), wins[g][:].bitcast(F32)[:, t, :])
+
+        def win_copies(g):
             wgrp = early.tile([P, 2, 512, 4], BF16, name="wgrp", tag="wgrp", align_bytes=64)
             wgrps[g] = wgrp
             for t in range(4):
-                transpose_words(
-                    win[:].bitcast(F32)[:, t, :],
-                    wgrp[:].bitcast(F32)[:, :, P * t : P * (t + 1), :],
-                )
+                copy_words((g, t), wgrp[:].bitcast(F32)[:, :, P * t : P * (t + 1), :])
 
-        def stage_b(g):
-            wgrp = wgrps[g]
-            wq = early.tile([P, 2, 512], U32, name="wq", align_bytes=64)
-            wqs = early.tile([P, 2, 512], U8, name="wqs", align_bytes=64)
+        def win_codes(g):
+            wq = early.tile([P, 2, 512], U32, name="wq", align_bytes=64, bufs=1)
+            wsc = early.tile([P, 2, 512], U8, name="wsc", align_bytes=64, bufs=1)
+            wqs[g] = (wq, wsc)
             nc.vector.quantize_mx(
                 out=wq[:].rearrange("p c w -> p (c w)").bitcast(FP8X4),
-                scales=wqs[:].rearrange("p c w -> p (c w)"),
-                in_=wgrp[:].rearrange("p c w t -> p (c w t)"),
+                scales=wsc[:].rearrange("p c w -> p (c w)"),
+                in_=wgrps[g][:].rearrange("p c w t -> p (c w t)"),
             )
-            stb = early.tile([P, 4, M], BF16, name="stb")
-            stbs[g] = stb
+
+        def state_passes(g):
+            wq, wsc = wqs[g]
             for half in range(2):
                 st = bank(2 + half, [P, 2, M], "st_ps")
+                sts[(g, half)] = st
                 for tt in range(2):
                     t = 2 * half + tt
                     for c in range(2):
                         nc.tensor.matmul_mx(
                             out=st[:, tt, :],
                             lhsT=wq[:, c, P * t : P * (t + 1)].bitcast(FP8X4),
-                            lhsT_scale=wqs[:, c, P * t : P * (t + 1)],
+                            lhsT_scale=wsc[:, c, P * t : P * (t + 1)],
                             rhs=xq[:, c, :].bitcast(FP8X4),
                             rhs_scale=xqs[:, c, :],
                             start=(c == 0),
                             stop=(c == 1),
                         )
-                for tt in range(2):
-                    t = 2 * half + tt
-                    i = 4 * g + t
-                    nc.scalar.activation(
-                        out=stb[:, t, :], in_=st[:, tt, :], func=ACT.Identity, bias=bias_f[:, i : i + 1]
-                    )
-                    nc.scalar.activation(
-                        out=sT[:, i, :], in_=st[:, tt, :], func=ACT.Tanh, bias=bias_f[:, i : i + 1]
-                    )
 
-        def stage_c(g):
-            stb = stbs[g]
+        def state_out(g):
+            stb = early.tile([P, 4, M], BF16, name="stb")
+            stbs[g] = stb
+            for t in range(4):
+                i = 4 * g + t
+                st = sts[(g, t // 2)]
+                bias = bias_f[:, i : i + 1]
+                nc.scalar.activation(out=stb[:, t, :], in_=st[:, t % 2, :], func=ACT.Identity, bias=bias)
+                nc.scalar.activation(out=sT[:, i, :], in_=st[:, t % 2, :], func=ACT.Tanh, bias=bias)
+
+        gsts = {}
+
+        def state_regroup(g):
             gst = early.tile([P, 2, M, 4], BF16, name="gst", align_bytes=64)
-            nc.vector.tensor_copy(out=gst[:, 0], in_=stb[:].rearrange("p t m -> p m t"))
+            gsts[g] = gst
+            nc.vector.tensor_copy(out=gst[:, 0], in_=stbs[g][:].rearrange("p t m -> p m t"))
             nc.vector.tensor_copy(
                 out=gst[:, 1], in_=sT[:, 4 * g : 4 * (g + 1), :].rearrange("p t m -> p m t")
             )
+
+        def state_codes(g):
             nc.vector.quantize_mx(
                 out=stq[:, g].rearrange("p a m -> p (a m)").bitcast(FP8X4),
                 scales=stqs[:, g].rearrange("p a m -> p (a m)"),
-                in_=gst[:].rearrange("p a m t -> p (a m t)"),
+                in_=gsts[g][:].rearrange("p a m t -> p (a m t)"),
             )
 
-        codes = const.tile([P, 2, 4, 2, 512], U32, name="codes", align_bytes=64)
-        scl = const.tile([P, 2, 4, 2, 512], U8, name="scl", align_bytes=64)
-        noise = early.tile([P, 2, N], BF16, name="noise", tag="win", bufs=3)
-        eps = {}
-        nts = {}
+        codes = const.tile([P, 2, 4, 1024], U32, name="codes", align_bytes=64)
+        scl = const.tile([P, 2, 4, 1024], U8, name="scl", align_bytes=64)
+        noises = []
+
+        def load_noise():
+            noise = early.tile([P, 2, N], BF16, name="noise", tag="win", bufs=3)
+            nc.sync.dma_start(out=noise[:], in_=noise_raw.rearrange("(t p) n -> p t n", p=P))
+            noises.append(noise)
+
+        prods = {}
+        grps = {}
+
+        def regroup(engine_copy, i, c0, c1):
+            prod, first = prods[i]
+            engine_copy(
+                out=grps[i][:, c0:c1, :].rearrange("p (c i) t -> p c t i", i=4),
+                in_=prod[:, :, first + c0 : first + c1].rearrange("p t (c i) -> p c t i", i=4),
+            )
+
+        def product(i):
+            s, a, c0, c1 = UNITS[i]
+            grps[i] = work.tile([P, 1024, 4], BF16, name="grp", align_bytes=64)
+            if i > LAST_PRODUCT:
+                prods[i] = (prods[LAST_PRODUCT][0], c0)
+                return
+            if i == LAST_PRODUCT:
+                c1 = 1024
+            prod = work.tile([P, 4, 1024], BF16, name="prod")
+            prods[i] = (prod, 0)
+            nc.vector.tensor_tensor(
+                out=prod[:, :, : c1 - c0],
+                in0=sets[(s, "j" if a == 1 else "w")][:, :, c0:c1],
+                in1=sets[(s, "m")][:, :, c0:c1],
+                op=ALU.mult,
+            )
+            if c1 == 1024 and a == 1 and s + 2 < 8:
+                load_cols(s + 2, "j", 0, 1024)
+            if c1 == 1024 and a == 0 and s + 2 < 8:
+                load_cols(s + 2, "w", 0, 1024)
+                if s + 3 < 8:
+                    load_cols(s + 3, "m", 0, 1024)
+
+        def scalar_regroup(i):
+            s, a, c0, c1 = UNITS[i]
+            regroup(nc.scalar.copy, i, 0, c1 - c0 - VECTOR_COLS.get(i, 0))
+
+        def vector_regroup(i):
+            s, a, c0, c1 = UNITS[i]
+            if i in VECTOR_COLS:
+                regroup(nc.vector.tensor_copy, i, c1 - c0 - VECTOR_COLS[i], c1 - c0)
 
         accs = {}
+        ready = {}
 
-        def transpose_noise(h, a, nb):
-            i0 = 8 * h + 4 * nb
+        def passes(h, a, pair, g):
+            acc = accs[(h, a, pair)]
+            for c2 in range(2):
+                c = 2 * pair + c2
+                nc.tensor.matmul_mx(
+                    out=acc[:, c2, :],
+                    lhsT=codes[:, a, g, P * c : P * (c + 1)].bitcast(FP8X4),
+                    lhsT_scale=scl[:, a, g, P * c : P * (c + 1)],
+                    rhs=stq[:, g, a, :].bitcast(FP8X4),
+                    rhs_scale=stqs[:, g, a, :],
+                    start=(g == 0 and c2 == 0),
+                    stop=(g == 3 and c2 == 1),
+                )
+
+        def open_pair(h, a, pair):
+            accs[(h, a, pair)] = bank(PAIR_BANKS[(h, a)][pair], [P, 2, M], "acc")
+            for g in ready.get((h, a, pair), []):
+                passes(h, a, pair, g)
+
+        def quantise(i):
+            s, a, c0, c1 = UNITS[i]
+            h, g = divmod(s, 4)
+            nc.vector.quantize_mx(
+                out=codes[:, a, g, c0:c1].bitcast(FP8X4),
+                scales=scl[:, a, g, c0:c1],
+                in_=grps[i][:, : c1 - c0, :].rearrange("p n t -> p (n t)"),
+            )
+            for pair in range(c0 // 256, c1 // 256):
+                if (h, a, pair) in accs:
+                    passes(h, a, pair, g)
+                else:
+                    ready.setdefault((h, a, pair), []).append(g)
+
+        nts = {}
+        eps = {}
+        ots = {}
+        outs = {}
+
+        def noise_transposes(h, nb):
             n_t = bank(NOISE_BANKS[nb], [P, 4, M], "n_t", BF16)
             nts[(h, nb)] = n_t
             for c in range(4):
+                i = 8 * h + 4 * nb + c
                 for mt in range(2):
                     nc.tensor.transpose(
                         n_t[:, c, P * mt : P * (mt + 1)],
-                        noise[:, mt, P * (i0 + c) : P * (i0 + c + 1)],
+                        noises[0][:, mt, P * i : P * (i + 1)],
                         ident_b[:],
                     )
-            if h == 1:
-                n_sb = work.tile([P, 4, M], BF16, name="n_sb", bufs=2)
-                nc.scalar.copy(out=n_sb[:], in_=n_t[:])
-                nts[(h, nb)] = n_sb
-                if nb == 1:
-                    open_group(1, 1, 1)
 
-        waiting = {}
+        def noise_out(h, nb):
+            n_sb = work.tile([P, 4, M], BF16, name="n_sb", bufs=2)
+            nc.scalar.copy(out=n_sb[:], in_=nts[(h, nb)][:])
+            nts[(h, nb)] = n_sb
 
-        def passes(h, a, nb, g):
-            for q in range(2):
-                acc = accs[(h, a, nb)][q]
-                for c2 in range(2):
-                    c = 2 * q + c2
-                    nc.tensor.matmul_mx(
-                        out=acc[:, c2, :],
-                        lhsT=codes[:, a, g, nb, P * c : P * (c + 1)].bitcast(FP8X4),
-                        lhsT_scale=scl[:, a, g, nb, P * c : P * (c + 1)],
-                        rhs=stq[:, g, a, :].bitcast(FP8X4),
-                        rhs_scale=stqs[:, g, a, :],
-                        start=(g == 0 and c2 == 0),
-                        stop=(g == 3 and c2 == 1),
-                    )
-
-        def open_group(h, a, nb):
-            banks = GROUP_BANKS[(h, a, nb)]
-            acc0 = bank(banks[0], [P, 2, M], "acc")
-            acc1 = bank(banks[1], [P, 2, M], "acc")
-            accs[(h, a, nb)] = (acc0, acc1)
-            for g in waiting.get((h, a, nb), []):
-                passes(h, a, nb, g)
-
-        def codes_ready(h, a, nb, g):
-            if (h, a, nb) in accs:
-                passes(h, a, nb, g)
-            else:
-                waiting[(h, a, nb)] = waiting.get((h, a, nb), []) + [g]
-
-        def finish(h, a, nb):
-            i0 = 8 * h + 4 * nb
-            if a == 1:
+        def end_delta(h, pair):
+            nb, q = divmod(pair, 2)
+            if q == 0:
                 eps[(h, nb)] = early.tile([P, 4, M], F32, name="ep", tag="wgrp", align_bytes=64)
             ep = eps[(h, nb)]
-            n_t = nts[(h, nb)]
-            for q in range(2):
-                acc = accs[(h, a, nb)][q]
-                pair = slice(2 * q, 2 * q + 2)
-                if a == 1:
-                    nc.vector.scalar_tensor_tensor(
-                        out=ep[:, pair, :],
-                        in0=acc[:],
-                        scalar=lam_f[:, 0:1],
-                        in1=sT[:, i0 + 2 * q : i0 + 2 * q + 2, :],
-                        op0=ALU.mult,
-                        op1=ALU.mult,
-                    )
-                    for c2 in range(2):
-                        c = 2 * q + c2
-                        nc.vector.scalar_tensor_tensor(
-                            out=ep[:, c, :],
-                            in0=n_t[:, c, :],
-                            scalar=t_f[:, i0 + c : i0 + c + 1],
-                            in1=ep[:, c, :],
-                            op0=ALU.mult,
-                            op1=ALU.add,
-                        )
-                else:
-                    nc.vector.tensor_tensor(
-                        out=ep[:, pair, :], in0=acc[:], in1=ep[:, pair, :], op=ALU.add
-                    )
-            if a == 0:
-                for mt in range(2):
-                    ot = bank(mt, [P, 4, P], "ot")
-                    for c in range(4):
-                        nc.tensor.transpose(ot[:, c, :], ep[:, c, P * mt : P * (mt + 1)], ident[:])
-                    o_t = early.tile([P, 512], F32, name="o_t", tag="gst", align_bytes=64)
-                    nc.scalar.activation(
-                        out=o_t[:], in_=ot[:].rearrange("p c r -> p (c r)"), func=ACT.Tanh
-                    )
-                    nc.sync.dma_start(
-                        out=out[P * mt : P * (mt + 1), P * i0 : P * (i0 + 4)], in_=o_t[:]
-                    )
-            if a == 0 and h == 0:
-                open_group(1, 0, nb)
-                if nb == 1:
-                    open_group(1, 1, 0)
+            i0 = 8 * h + 2 * pair
+            nc.vector.scalar_tensor_tensor(
+                out=ep[:, 2 * q : 2 * q + 2, :],
+                in0=accs[(h, 1, pair)][:],
+                scalar=lam_f[:, 0:1],
+                in1=sT[:, i0 : i0 + 2, :],
+                op0=ALU.mult,
+                op1=ALU.mult,
+            )
+            for c2 in range(2):
+                c = 2 * q + c2
+                nc.vector.scalar_tensor_tensor(
+                    out=ep[:, c, :],
+                    in0=nts[(h, nb)][:, c, :],
+                    scalar=t_f[:, i0 + c2 : i0 + c2 + 1],
+                    in1=ep[:, c, :],
+                    op0=ALU.mult,
+                    op1=ALU.add,
+                )
 
-        def regroup(engine_copy, grp, prod, c0, c1):
-            engine_copy(
-                out=grp[:, c0:c1, :].rearrange("p (c i) t -> p c t i", i=4),
-                in_=prod[:, :, c0:c1].rearrange("p t (c i) -> p c t i", i=4),
+        def end_signal(h, pair):
+            nb, q = divmod(pair, 2)
+            ep = eps[(h, nb)][:, 2 * q : 2 * q + 2, :]
+            nc.vector.tensor_tensor(out=ep, in0=accs[(h, 0, pair)][:], in1=ep, op=ALU.add)
+
+        def out_transposes(h, pair):
+            nb, q = divmod(pair, 2)
+            ot = bank(OUT_BANKS[h][pair], [P, 2, 2, P], "ot")
+            ots[(h, pair)] = ot
+            for mt in range(2):
+                for c2 in range(2):
+                    nc.tensor.transpose(
+                        ot[:, mt, c2, :],
+                        eps[(h, nb)][:, 2 * q + c2, P * mt : P * (mt + 1)],
+                        ident[:],
+                    )
+
+        def store(h, pair):
+            nb, q = divmod(pair, 2)
+            if q == 0:
+                outs[(h, nb)] = early.tile([P, 2, 2, 256], F32, name="o_t", tag="gst", align_bytes=64)
+            o_t = outs[(h, nb)][:, q]
+            nc.scalar.activation(
+                out=o_t, in_=ots[(h, pair)][:].rearrange("p m c r -> p m (c r)"), func=ACT.Tanh
+            )
+            c0 = 1024 * h + 256 * pair
+            nc.sync.dma_start(
+                out=out[:, c0 : c0 + 256].rearrange("(m p) n -> p m n", p=P), in_=o_t
             )
 
-        def unit(s, a, c0, c1):
-            g = s % 4
-            width = c1 - c0
-            src = sets[(s, "j" if a == 1 else "w")]
-            m_t = sets[(s, "m")]
-            prod = work.tile([P, 4, 1024], BF16, name="prod")
-            nc.vector.tensor_tensor(
-                out=prod[:, :, :width], in0=src[:, :, c0:c1], in1=m_t[:, :, c0:c1], op=ALU.mult
-            )
-            grp = work.tile([P, 1024, 4], BF16, name="grp", align_bytes=64)
-            split = width - (width // 4 if a == 1 else 0)
-            regroup(nc.scalar.copy, grp, prod, 0, split)
-            if split < width:
-                regroup(nc.vector.tensor_copy, grp, prod, split, width)
-            nc.vector.quantize_mx(
-                out=codes[:, a, g].rearrange("p b n -> p (b n)")[:, c0:c1].bitcast(FP8X4),
-                scales=scl[:, a, g].rearrange("p b n -> p (b n)")[:, c0:c1],
-                in_=grp[:, :width, :].rearrange("p n t -> p (n t)"),
-            )
-            for nb in range(2):
-                if c0 < 512 * (nb + 1) <= c1:
-                    codes_ready(s // 4, a, nb, g)
+        before = {}
+        after = {}
 
-        load_one(0, "w")
-        load_win(1)
-        load_one(1, "m")
-        load_one(1, "j")
-        load_win(2)
-        load_one(1, "w")
-        load_win(3)
+        def put(where, index, job, *args):
+            where.setdefault(index, []).append((job, args))
 
-        first_stage = {
-            1: [stage_x, lambda: stage_a(0)],
-            2: [lambda: stage_b(0)],
-            3: [lambda: stage_a(1), lambda: stage_c(0)],
-            4: [lambda: stage_b(1)],
-            5: [lambda: stage_a(2), lambda: stage_c(1)],
-            6: [lambda: stage_b(2)],
-            7: [lambda: stage_a(3), lambda: stage_c(2)],
-            8: [lambda: stage_b(3)],
-            9: [lambda: stage_c(3), finish_t],
-        }
-        jobs = {}
+        put(before, 0, x_transposes)
+        put(after, 0, x_copies)
+        put(after, 1, small_vectors)
+        put(after, 1, x_codes)
+        put(after, 1, win_transposes, 0)
+        for g, index in enumerate((2, 3, 5, 6)):
+            put(after, index, win_copies, g)
+            if g < 3:
+                put(after, (2, 4, 5)[g], win_transposes, g + 1)
+        for g, index in enumerate((3, 4, 6, 7)):
+            put(before, index, win_codes, g)
+            put(before, index, state_passes, g)
+        for g, index in enumerate((4, 5, 7, 8)):
+            put(before, index, state_out, g)
+        for g, index in enumerate((5, 6, 8, 9)):
+            put(before, index, state_regroup, g)
+            put(after, index, state_codes, g)
+        put(after, 7, load_noise)
+        put(after, 9, finish_t)
+        for nb in range(2):
+            put(after, 10, noise_transposes, 0, nb)
+        for pair in range(4):
+            put(after, 10, open_pair, 0, 1, pair)
+            put(after, 11 + pair // 2, end_delta, 0, pair)
+        for pair in range(4):
+            put(after, 11, open_pair, 0, 0, pair)
+            put(after, 13, end_signal, 0, pair)
+        for pair in range(4):
+            put(after, 14 + pair // 2, store, 0, pair)
+        for pair in range(4):
+            put(after, 13 + pair // 2, out_transposes, 0, pair)
+            put(after, 14 + pair // 2, open_pair, 1, 1, pair)
+            put(after, 16 + pair // 2, end_delta, 1, pair)
+        for nb in range(2):
+            put(after, 12, noise_transposes, 1, nb)
+            put(after, 13, noise_out, 1, nb)
+        for pair in range(4):
+            put(after, 15, open_pair, 1, 0, pair)
+        for pair, index in ((0, 19), (1, 19), (2, 20), (3, 21)):
+            put(after, index, end_signal, 1, pair)
+            put(after, index, out_transposes, 1, pair)
+        for pair, index in ((0, 20), (1, 20), (2, 21), (3, 21)):
+            put(after, index, store, 1, pair)
 
-        def later(index, job):
-            jobs[index] = jobs.get(index, []) + [job]
+        def run(jobs):
+            for job, args in jobs:
+                job(*args)
 
-        def run_jobs(index):
-            for job in jobs.get(index, []):
-                job[0](job[1], job[2], job[3])
-
-        for h in range(2):
-            for nb in range(2):
-                later(NOISE_AT[h] + nb, (transpose_noise, h, 1, nb))
-
-        count = 0
-        for s in range(8):
-            h = s // 4
-            for a in (1, 0):
-                fine = FINE.get(count)
-                for nb in range(2):
-                    for job in first_stage.get(count, []):
-                        job()
-                    if count == 9:
-                        nc.sync.dma_start(
-                            out=noise[:], in_=noise_raw.rearrange("(t p) n -> p t n", p=P)
-                        )
-                    if fine:
-                        for c0, c1 in fine[nb]:
-                            unit(s, a, c0, c1)
-                    elif nb == 0:
-                        unit(s, a, 0, 1024)
-                    if nb == 1 and s + 2 < 8:
-                        if a == 1:
-                            load_one(s + 2, "j")
-                        else:
-                            load_one(s + 2, "m")
-                            load_one(s + 2, "w")
-                    if s % 4 == 3:
-                        if h == 0:
-                            later(count + OPEN_LAG, (open_group, h, a, nb))
-                        later(count + LAGS[(h, a)], (finish, h, a, nb))
-                    run_jobs(count)
-                    count += 1
-        for index in range(count, count + 8):
-            run_jobs(index)
+        last = len(UNITS) - 1
+        product(0)
+        for i in range(last + 2):
+            run(before.get(i, []))
+            if i < last:
+                product(i + 1)
+            if i <= last:
+                scalar_regroup(i)
+            if i > 0:
+                quantise(i - 1)
+            if i < last:
+                vector_regroup(i + 1)
+            run(after.get(i, []))

@@ -27,7 +27,9 @@ UNITS = UNITS + [(s, a, 0, 1024) for s in range(1, 5) for a in (1, 0)]
 UNITS = UNITS + [(5, 1, 0, 1024), (6, 1, 0, 1024), (7, 1, 0, 1024), (5, 0, 0, 1024), (6, 0, 0, 1024)]
 UNITS = UNITS + [(7, 0, 0, 512), (7, 0, 512, 768), (7, 0, 768, 1024)]
 LAST_PRODUCT = len(UNITS) - 3
-VECTOR_COLS = {5: 512, 6: 512, 7: 512, 8: 512, 9: 256}
+VECTOR_COLS = {5: 256, 6: 256, 7: 256, 8: 256}
+TENSOR_COLS = {4: 512, 5: 512, 6: 512, 7: 512, 8: 512, 9: 512, 10: 512}
+REGROUP_BANKS = (4, 5)
 PAIR_BANKS = {(0, 1): (4, 5, 6, 2), (0, 0): (0, 1, 4, 5), (1, 1): (4, 5, 6, 2), (1, 0): (0, 1, 7, 3)}
 NOISE_BANKS = (7, 3)
 TRANSPOSE_BANKS = (0, 1, 6, 7)
@@ -310,9 +312,32 @@ def tile_brainquantumlayer_pa_kernel(
                 if s + 3 < 8:
                     load_cols(s + 3, "m", 0, 1024)
 
+        regrouped = {}
+
+        def tensor_regroup(i):
+            prod, first = prods[i]
+            for b in range(TENSOR_COLS.get(i, 0) // 256):
+                ps = bank(REGROUP_BANKS[b], [P, 256, 4], "rg_ps", BF16)
+                regrouped[(i, b)] = ps
+                for j in range(2):
+                    c = first + 256 * b + 128 * j
+                    nc.tensor.matmul(
+                        out=ps[:, 128 * j : 128 * (j + 1), :].rearrange("p (c i) t -> p c t i", i=4),
+                        lhsT=ident_b[:],
+                        rhs=prod[:, :, c : c + 128].rearrange("p t (c i) -> p c t i", i=4),
+                        start=True,
+                        stop=True,
+                    )
+
+        def regrouped_out(i):
+            for b in range(TENSOR_COLS.get(i, 0) // 256):
+                nc.scalar.copy(out=grps[i][:, 256 * b : 256 * (b + 1), :], in_=regrouped[(i, b)][:])
+
         def scalar_regroup(i):
             s, a, c0, c1 = UNITS[i]
-            regroup(nc.scalar.copy, i, 0, c1 - c0 - VECTOR_COLS.get(i, 0))
+            first, end = TENSOR_COLS.get(i, 0), c1 - c0 - VECTOR_COLS.get(i, 0)
+            if end > first:
+                regroup(nc.scalar.copy, i, first, end)
 
         def vector_regroup(i):
             s, a, c0, c1 = UNITS[i]
@@ -490,8 +515,11 @@ def tile_brainquantumlayer_pa_kernel(
         product(0)
         for i in range(last + 2):
             run(before.get(i, []))
+            if i <= last:
+                regrouped_out(i)
             if i < last:
                 product(i + 1)
+                tensor_regroup(i + 1)
             if i <= last:
                 scalar_regroup(i)
             if i > 0:

@@ -30,6 +30,8 @@ LAST_PRODUCT = len(UNITS) - 3
 VECTOR_COLS = {5: 256, 6: 256, 7: 256, 8: 256}
 TENSOR_COLS = {4: 512, 5: 512, 6: 512, 7: 512, 8: 512, 9: 512, 10: 512}
 REGROUP_BANKS = (4, 5)
+SCALAR_RUN = 8
+VECTOR_RUN = 4
 PAIR_BANKS = {(0, 1): (4, 5, 6, 2), (0, 0): (0, 1, 4, 5), (1, 1): (4, 5, 6, 2), (1, 0): (0, 1, 7, 3)}
 NOISE_BANKS = (7, 3)
 TRANSPOSE_BANKS = (0, 1, 6, 7)
@@ -282,11 +284,11 @@ def tile_brainquantumlayer_pa_kernel(
         prods = {}
         grps = {}
 
-        def regroup(engine_copy, i, c0, c1):
+        def regroup(engine_copy, i, c0, c1, run):
             prod, first = prods[i]
             engine_copy(
-                out=grps[i][:, c0:c1, :].rearrange("p (c i) t -> p c t i", i=4),
-                in_=prod[:, :, first + c0 : first + c1].rearrange("p t (c i) -> p c t i", i=4),
+                out=grps[i][:, c0:c1, :].rearrange("p (c i) t -> p c t i", i=run),
+                in_=prod[:, :, first + c0 : first + c1].rearrange("p t (c i) -> p c t i", i=run),
             )
 
         def product(i):
@@ -337,12 +339,12 @@ def tile_brainquantumlayer_pa_kernel(
             s, a, c0, c1 = UNITS[i]
             first, end = TENSOR_COLS.get(i, 0), c1 - c0 - VECTOR_COLS.get(i, 0)
             if end > first:
-                regroup(nc.scalar.copy, i, first, end)
+                regroup(nc.scalar.copy, i, first, end, SCALAR_RUN)
 
         def vector_regroup(i):
             s, a, c0, c1 = UNITS[i]
             if i in VECTOR_COLS:
-                regroup(nc.vector.tensor_copy, i, c1 - c0 - VECTOR_COLS[i], c1 - c0)
+                regroup(nc.vector.tensor_copy, i, c1 - c0 - VECTOR_COLS[i], c1 - c0, VECTOR_RUN)
 
         accs = {}
         ready = {}
@@ -501,7 +503,7 @@ def tile_brainquantumlayer_pa_kernel(
             put(after, 13, noise_out, 1, nb)
         for pair in range(4):
             put(after, 15, open_pair, 1, 0, pair)
-        for pair, index in ((0, 19), (1, 19), (2, 20), (3, 21)):
+        for pair, index in ((0, 20), (1, 20), (2, 21), (3, 21)):
             put(after, index, end_signal, 1, pair)
             put(after, index, out_transposes, 1, pair)
         for pair, index in ((0, 20), (1, 20), (2, 21), (3, 21)):
@@ -515,13 +517,13 @@ def tile_brainquantumlayer_pa_kernel(
         product(0)
         for i in range(last + 2):
             run(before.get(i, []))
-            if i <= last:
-                regrouped_out(i)
             if i < last:
                 product(i + 1)
-                tensor_regroup(i + 1)
             if i <= last:
                 scalar_regroup(i)
+                regrouped_out(i)
+            if i < last:
+                tensor_regroup(i + 1)
             if i > 0:
                 quantise(i - 1)
             if i < last:

from contextlib import ExitStack
import math

import concourse.mybir as mybir
from concourse.masks import make_identity

F32 = mybir.dt.float32
BF16 = mybir.dt.bfloat16
U32 = mybir.dt.uint32
U8 = mybir.dt.uint8
I32 = mybir.dt.int32
FP8X4 = mybir.dt.float8_e4m3fn_x4
ACT = mybir.ActivationFunctionType
ALU = mybir.AluOpType

P = 128
M, DI, N = 256, 1024, 2048
FLOPS = 2 * M * DI * N + 2 * 2 * M * N * N

PI_HI = 3.140625
PI_LO = math.pi - PI_HI
TAYLOR = [(-1.0) ** k / math.factorial(2 * k + 1) for k in range(9)]


UNITS = [(0, 1, 0, 256), (0, 1, 256, 512), (0, 1, 512, 1024), (0, 0, 0, 512), (0, 0, 512, 1024)]
UNITS = UNITS + [(s, a, 0, 1024) for s in range(1, 5) for a in (1, 0)]
UNITS = UNITS + [(5, 1, 0, 1024), (6, 1, 0, 1024), (7, 1, 0, 1024), (5, 0, 0, 1024), (6, 0, 0, 1024)]
UNITS = UNITS + [(7, 0, 0, 512), (7, 0, 512, 768), (7, 0, 768, 1024)]
LAST_PRODUCT = len(UNITS) - 3
VECTOR_COLS = {5: 256, 6: 256, 7: 256, 8: 256}
TENSOR_COLS = {4: 512, 5: 512, 6: 512, 7: 512, 8: 512, 9: 512, 10: 512}
REGROUP_BANKS = (4, 5)
SCALAR_RUN = 8
VECTOR_RUN = 4
PAIR_BANKS = {(0, 1): (4, 5, 6, 2), (0, 0): (0, 1, 4, 5), (1, 1): (4, 5, 6, 2), (1, 0): (0, 1, 7, 3)}
NOISE_BANKS = (7, 3)
TRANSPOSE_BANKS = (0, 1, 6, 7)
OUT_BANKS = {0: (6, 2, 6, 2), 1: (4, 5, 6, 2)}


def tile_brainquantumlayer_pa_kernel(
    tc, x, W_in, b_in, weights, J, theta, lam, mask, noise_raw, out
):
    nc = tc.nc
    with ExitStack() as ctx:
        const = ctx.enter_context(tc.tile_pool(name="const", bufs=1))
        early = ctx.enter_context(tc.tile_pool(name="early", bufs=2))
        stream = ctx.enter_context(tc.tile_pool(name="stream", bufs=2))
        work = ctx.enter_context(tc.tile_pool(name="work", bufs=3))
        psum = ctx.enter_context(tc.psum_pool(name="psum", bufs=1))
        ctx.enter_context(
            tc.manual_schedule(
                engines={mybir.EngineType.PE, mybir.EngineType.Activation, mybir.EngineType.DVE}
            )
        )

        def bank(i, shape, name, dtype=F32):
            return psum.tile(shape, dtype, tag="bank%d" % i, name=name)

        sets = {}

        def load_cols(s, kind, c0, c1):
            h, g = divmod(s, 4)
            src = {"m": mask, "j": J, "w": weights}[kind]
            if c0 == 0:
                t_in = stream.tile(
                    [P, 4, 1024], BF16, name="in_" + kind, tag="in_" + kind, bufs=3 if kind == "m" else 2
                )
                sets[(s, kind)] = t_in
            nc.sync.dma_start(
                out=sets[(s, kind)][:, :, c0:c1],
                in_=src[512 * g : 512 * (g + 1), 1024 * h + c0 : 1024 * h + c1].rearrange(
                    "(t p) n -> p t n", p=P
                ),
            )

        wins = {}

        def load_win(g):
            win = early.tile([P, 4, DI], BF16, name="win", tag="win", bufs=3)
            nc.sync.dma_start(
                out=win[:], in_=W_in[512 * g : 512 * (g + 1), :].rearrange("(t p) k -> p t k", p=P)
            )
            wins[g] = win

        load_cols(0, "m", 0, 256)
        load_cols(0, "j", 0, 256)
        x_sb = early.tile([P, 2, DI], BF16, name="x_sb", tag="win", bufs=3)
        nc.sync.dma_start(out=x_sb[:], in_=x.rearrange("(t p) k -> p t k", p=P))
        load_cols(0, "m", 256, 512)
        load_cols(0, "j", 256, 512)
        load_cols(0, "m", 512, 1024)
        load_cols(0, "j", 512, 1024)
        load_win(0)
        load_cols(0, "w", 0, 1024)
        load_win(1)
        load_cols(1, "m", 0, 1024)
        load_cols(1, "j", 0, 1024)
        load_win(2)
        load_cols(1, "w", 0, 1024)
        load_win(3)
        load_cols(2, "m", 0, 1024)

        dummy = const.tile([P, 1], F32, name="dummy")
        nc.vector.memset(dummy[:], 0.0)
        warm = const.tile([P, 1], F32, name="warm")
        nc.scalar.activation(out=warm[:], in_=dummy[:], func=ACT.Tanh)
        ident = const.tile([P, P], F32, name="ident")
        make_identity(nc, ident[:])
        ident_b = const.tile([P, P], BF16, name="ident_b")
        make_identity(nc, ident_b[:])

        vecs = const.tile([P, P], BF16, name="vecs")
        nc.vector.memset(vecs[:], 0.0)
        nc.scalar.dma_start(out=vecs[0:16, :], in_=b_in.rearrange("(i p) -> i p", p=P))
        nc.scalar.dma_start(out=vecs[16:32, :], in_=theta.rearrange("(i p) -> i p", p=P))
        lam_b = const.tile([P, 1], BF16, name="lam_b")
        nc.scalar.dma_start(out=lam_b[:], in_=lam.partition_broadcast(P))
        vec_f = const.tile([P, 32], F32, name="vec_f")
        bias_f = vec_f[:, 0:16]
        lam_f = const.tile([P, 1], F32, name="lam_f")
        s01 = const.tile([P, 16], F32, name="s01")
        t_f = const.tile([P, 16], F32, name="t_f")

        def small_vectors():
            vps = bank(2, [P, P], "vps", BF16)
            nc.tensor.transpose(vps[:], vecs[:], ident_b[:])
            nc.vector.tensor_copy(out=vec_f[:], in_=vps[:, 0:32])
            nc.vector.tensor_copy(out=lam_f[:], in_=lam_b[:])
            th_f = vec_f[:, 16:32]
            tq = const.tile([P, 16], F32, name="tq")
            nc.vector.tensor_scalar_mul(out=tq[:], in0=th_f, scalar1=2.0 / math.pi)
            ni = const.tile([P, 16], I32, name="ni")
            nc.vector.tensor_copy(out=ni[:], in_=tq[:])
            nf = const.tile([P, 16], F32, name="nf")
            nc.vector.tensor_copy(out=nf[:], in_=ni[:])
            y2 = const.tile([P, 16], F32, name="y2")
            nc.vector.tensor_scalar_mul(out=y2[:], in0=th_f, scalar1=2.0)
            r1 = const.tile([P, 16], F32, name="r1")
            nc.vector.scalar_tensor_tensor(
                out=r1[:], in0=nf[:], scalar=-PI_HI, in1=y2[:], op0=ALU.mult, op1=ALU.add
            )
            r2 = const.tile([P, 16], F32, name="r2")
            nc.vector.scalar_tensor_tensor(
                out=r2[:], in0=nf[:], scalar=-PI_LO, in1=r1[:], op0=ALU.mult, op1=ALU.add
            )
            sq = const.tile([P, 16], F32, name="sq")
            nc.gpsimd.tensor_tensor(out=sq[:], in0=r2[:], in1=r2[:], op=ALU.mult)
            poly = const.tile([P, 16], F32, name="poly")
            nc.gpsimd.tensor_scalar(
                out=poly[:], in0=sq[:], scalar1=TAYLOR[8], scalar2=TAYLOR[7], op0=ALU.mult, op1=ALU.add
            )
            for k in range(6, -1, -1):
                nc.gpsimd.tensor_tensor(out=poly[:], in0=poly[:], in1=sq[:], op=ALU.mult)
                nc.gpsimd.tensor_scalar(
                    out=poly[:], in0=poly[:], scalar1=1.0, scalar2=TAYLOR[k], op0=ALU.mult, op1=ALU.add
                )
            nc.gpsimd.tensor_tensor(out=poly[:], in0=poly[:], in1=r2[:], op=ALU.mult)
            nc.gpsimd.tensor_scalar(
                out=s01[:], in0=poly[:], scalar1=0.1, scalar2=0.0, op0=ALU.mult, op1=ALU.add
            )

        def finish_t():
            nc.vector.scalar_tensor_tensor(
                out=t_f[:], in0=s01[:], scalar=-1.0, in1=s01[:], op0=ALU.mult, op1=ALU.max
            )

        tr_count = [0]
        tr_ps = {}

        def transpose_words(key, src_f32):
            i = TRANSPOSE_BANKS[tr_count[0] % len(TRANSPOSE_BANKS)]
            ps = bank(i, [P, 4, P], "tr_ps")
            tr_count[0] += 1
            tr_ps[key] = ps
            for q in range(4):
                nc.tensor.transpose(ps[:, q, :], src_f32[:, P * q : P * (q + 1)], ident[:])

        def copy_words(key, dst_f32):
            view = tr_ps[key][:].rearrange("p (c u) r -> p c r u", u=2)
            nc.scalar.copy(out=dst_f32, in_=view)

        xg = early.tile([P, 2, 2 * P, 4], BF16, name="xg", tag="wgrp", align_bytes=64)
        xq = const.tile([P, 2, 2 * P], U32, name="xq", align_bytes=64)
        xqs = const.tile([P, 2, 2 * P], U8, name="xqs", align_bytes=64)

        def x_transposes():
            for t in range(2):
                transpose_words(("x", t), x_sb[:].bitcast(F32)[:, t, :])

        def x_copies():
            for t in range(2):
                copy_words(("x", t), xg[:].bitcast(F32)[:, :, P * t : P * (t + 1), :])

        def x_codes():
            nc.vector.quantize_mx(
                out=xq[:].rearrange("p c w -> p (c w)").bitcast(FP8X4),
                scales=xqs[:].rearrange("p c w -> p (c w)"),
                in_=xg[:].rearrange("p c w t -> p (c w t)"),
            )

        stq = const.tile([P, 4, 2, M], U32, name="stq", align_bytes=64)
        stqs = const.tile([P, 4, 2, M], U8, name="stqs", align_bytes=64)
        sT = const.tile([P, 16, M], F32, name="sT")
        wgrps = {}
        wqs = {}
        sts = {}
        stbs = {}

        def win_transposes(g):
            for t in range(4):
                transpose_words((g, t), wins[g][:].bitcast(F32)[:, t, :])

        def win_copies(g):
            wgrp = early.tile([P, 2, 512, 4], BF16, name="wgrp", tag="wgrp", align_bytes=64)
            wgrps[g] = wgrp
            for t in range(4):
                copy_words((g, t), wgrp[:].bitcast(F32)[:, :, P * t : P * (t + 1), :])

        def win_codes(g):
            wq = early.tile([P, 2, 512], U32, name="wq", align_bytes=64, bufs=1)
            wsc = early.tile([P, 2, 512], U8, name="wsc", align_bytes=64, bufs=1)
            wqs[g] = (wq, wsc)
            nc.vector.quantize_mx(
                out=wq[:].rearrange("p c w -> p (c w)").bitcast(FP8X4),
                scales=wsc[:].rearrange("p c w -> p (c w)"),
                in_=wgrps[g][:].rearrange("p c w t -> p (c w t)"),
            )

        def state_passes(g):
            wq, wsc = wqs[g]
            for half in range(2):
                st = bank(2 + half, [P, 2, M], "st_ps")
                sts[(g, half)] = st
                for tt in range(2):
                    t = 2 * half + tt
                    for c in range(2):
                        nc.tensor.matmul_mx(
                            out=st[:, tt, :],
                            lhsT=wq[:, c, P * t : P * (t + 1)].bitcast(FP8X4),
                            lhsT_scale=wsc[:, c, P * t : P * (t + 1)],
                            rhs=xq[:, c, :].bitcast(FP8X4),
                            rhs_scale=xqs[:, c, :],
                            start=(c == 0),
                            stop=(c == 1),
                        )

        def state_out(g):
            stb = early.tile([P, 4, M], BF16, name="stb")
            stbs[g] = stb
            for t in range(4):
                i = 4 * g + t
                st = sts[(g, t // 2)]
                bias = bias_f[:, i : i + 1]
                nc.scalar.activation(out=stb[:, t, :], in_=st[:, t % 2, :], func=ACT.Identity, bias=bias)
                nc.scalar.activation(out=sT[:, i, :], in_=st[:, t % 2, :], func=ACT.Tanh, bias=bias)

        gsts = {}

        def state_regroup(g):
            gst = early.tile([P, 2, M, 4], BF16, name="gst", align_bytes=64)
            gsts[g] = gst
            nc.vector.tensor_copy(out=gst[:, 0], in_=stbs[g][:].rearrange("p t m -> p m t"))
            nc.vector.tensor_copy(
                out=gst[:, 1], in_=sT[:, 4 * g : 4 * (g + 1), :].rearrange("p t m -> p m t")
            )

        def state_codes(g):
            nc.vector.quantize_mx(
                out=stq[:, g].rearrange("p a m -> p (a m)").bitcast(FP8X4),
                scales=stqs[:, g].rearrange("p a m -> p (a m)"),
                in_=gsts[g][:].rearrange("p a m t -> p (a m t)"),
            )

        codes = const.tile([P, 2, 4, 1024], U32, name="codes", align_bytes=64)
        scl = const.tile([P, 2, 4, 1024], U8, name="scl", align_bytes=64)
        noises = []

        def load_noise():
            noise = early.tile([P, 2, N], BF16, name="noise", tag="win", bufs=3)
            nc.sync.dma_start(out=noise[:], in_=noise_raw.rearrange("(t p) n -> p t n", p=P))
            noises.append(noise)

        prods = {}
        grps = {}

        def regroup(engine_copy, i, c0, c1, run):
            prod, first = prods[i]
            engine_copy(
                out=grps[i][:, c0:c1, :].rearrange("p (c i) t -> p c t i", i=run),
                in_=prod[:, :, first + c0 : first + c1].rearrange("p t (c i) -> p c t i", i=run),
            )

        def product(i):
            s, a, c0, c1 = UNITS[i]
            grps[i] = work.tile([P, 1024, 4], BF16, name="grp", align_bytes=64)
            if i > LAST_PRODUCT:
                prods[i] = (prods[LAST_PRODUCT][0], c0)
                return
            if i == LAST_PRODUCT:
                c1 = 1024
            prod = work.tile([P, 4, 1024], BF16, name="prod")
            prods[i] = (prod, 0)
            nc.vector.tensor_tensor(
                out=prod[:, :, : c1 - c0],
                in0=sets[(s, "j" if a == 1 else "w")][:, :, c0:c1],
                in1=sets[(s, "m")][:, :, c0:c1],
                op=ALU.mult,
            )
            if c1 == 1024 and a == 1 and s + 2 < 8:
                load_cols(s + 2, "j", 0, 1024)
            if c1 == 1024 and a == 0 and s + 2 < 8:
                load_cols(s + 2, "w", 0, 1024)
                if s + 3 < 8:
                    load_cols(s + 3, "m", 0, 1024)

        regrouped = {}

        def tensor_regroup(i):
            prod, first = prods[i]
            for b in range(TENSOR_COLS.get(i, 0) // 256):
                ps = bank(REGROUP_BANKS[b], [P, 256, 4], "rg_ps", BF16)
                regrouped[(i, b)] = ps
                for j in range(2):
                    c = first + 256 * b + 128 * j
                    nc.tensor.matmul(
                        out=ps[:, 128 * j : 128 * (j + 1), :].rearrange("p (c i) t -> p c t i", i=4),
                        lhsT=ident_b[:],
                        rhs=prod[:, :, c : c + 128].rearrange("p t (c i) -> p c t i", i=4),
                        start=True,
                        stop=True,
                    )

        def regrouped_out(i):
            for b in range(TENSOR_COLS.get(i, 0) // 256):
                nc.scalar.copy(out=grps[i][:, 256 * b : 256 * (b + 1), :], in_=regrouped[(i, b)][:])

        def scalar_regroup(i):
            s, a, c0, c1 = UNITS[i]
            first, end = TENSOR_COLS.get(i, 0), c1 - c0 - VECTOR_COLS.get(i, 0)
            if end > first:
                regroup(nc.scalar.copy, i, first, end, SCALAR_RUN)

        def vector_regroup(i):
            s, a, c0, c1 = UNITS[i]
            if i in VECTOR_COLS:
                regroup(nc.vector.tensor_copy, i, c1 - c0 - VECTOR_COLS[i], c1 - c0, VECTOR_RUN)

        accs = {}
        ready = {}

        def passes(h, a, pair, g):
            acc = accs[(h, a, pair)]
            for c2 in range(2):
                c = 2 * pair + c2
                nc.tensor.matmul_mx(
                    out=acc[:, c2, :],
                    lhsT=codes[:, a, g, P * c : P * (c + 1)].bitcast(FP8X4),
                    lhsT_scale=scl[:, a, g, P * c : P * (c + 1)],
                    rhs=stq[:, g, a, :].bitcast(FP8X4),
                    rhs_scale=stqs[:, g, a, :],
                    start=(g == 0 and c2 == 0),
                    stop=(g == 3 and c2 == 1),
                )

        def open_pair(h, a, pair):
            accs[(h, a, pair)] = bank(PAIR_BANKS[(h, a)][pair], [P, 2, M], "acc")
            for g in ready.get((h, a, pair), []):
                passes(h, a, pair, g)

        def quantise(i):
            s, a, c0, c1 = UNITS[i]
            h, g = divmod(s, 4)
            nc.vector.quantize_mx(
                out=codes[:, a, g, c0:c1].bitcast(FP8X4),
                scales=scl[:, a, g, c0:c1],
                in_=grps[i][:, : c1 - c0, :].rearrange("p n t -> p (n t)"),
            )
            for pair in range(c0 // 256, c1 // 256):
                if (h, a, pair) in accs:
                    passes(h, a, pair, g)
                else:
                    ready.setdefault((h, a, pair), []).append(g)

        nts = {}
        eps = {}
        ots = {}
        outs = {}

        def noise_transposes(h, nb):
            n_t = bank(NOISE_BANKS[nb], [P, 4, M], "n_t", BF16)
            nts[(h, nb)] = n_t
            for c in range(4):
                i = 8 * h + 4 * nb + c
                for mt in range(2):
                    nc.tensor.transpose(
                        n_t[:, c, P * mt : P * (mt + 1)],
                        noises[0][:, mt, P * i : P * (i + 1)],
                        ident_b[:],
                    )

        def noise_out(h, nb):
            n_sb = work.tile([P, 4, M], BF16, name="n_sb", bufs=2)
            nc.scalar.copy(out=n_sb[:], in_=nts[(h, nb)][:])
            nts[(h, nb)] = n_sb

        def end_delta(h, pair):
            nb, q = divmod(pair, 2)
            if q == 0:
                eps[(h, nb)] = early.tile([P, 4, M], F32, name="ep", tag="wgrp", align_bytes=64)
            ep = eps[(h, nb)]
            i0 = 8 * h + 2 * pair
            nc.vector.scalar_tensor_tensor(
                out=ep[:, 2 * q : 2 * q + 2, :],
                in0=accs[(h, 1, pair)][:],
                scalar=lam_f[:, 0:1],
                in1=sT[:, i0 : i0 + 2, :],
                op0=ALU.mult,
                op1=ALU.mult,
            )
            for c2 in range(2):
                c = 2 * q + c2
                nc.vector.scalar_tensor_tensor(
                    out=ep[:, c, :],
                    in0=nts[(h, nb)][:, c, :],
                    scalar=t_f[:, i0 + c2 : i0 + c2 + 1],
                    in1=ep[:, c, :],
                    op0=ALU.mult,
                    op1=ALU.add,
                )

        def end_signal(h, pair):
            nb, q = divmod(pair, 2)
            ep = eps[(h, nb)][:, 2 * q : 2 * q + 2, :]
            nc.vector.tensor_tensor(out=ep, in0=accs[(h, 0, pair)][:], in1=ep, op=ALU.add)

        def out_transposes(h, pair):
            nb, q = divmod(pair, 2)
            ot = bank(OUT_BANKS[h][pair], [P, 2, 2, P], "ot")
            ots[(h, pair)] = ot
            for mt in range(2):
                for c2 in range(2):
                    nc.tensor.transpose(
                        ot[:, mt, c2, :],
                        eps[(h, nb)][:, 2 * q + c2, P * mt : P * (mt + 1)],
                        ident[:],
                    )

        def store(h, pair):
            nb, q = divmod(pair, 2)
            if q == 0:
                outs[(h, nb)] = early.tile([P, 2, 2, 256], F32, name="o_t", tag="gst", align_bytes=64)
            o_t = outs[(h, nb)][:, q]
            nc.scalar.activation(
                out=o_t, in_=ots[(h, pair)][:].rearrange("p m c r -> p m (c r)"), func=ACT.Tanh
            )
            c0 = 1024 * h + 256 * pair
            nc.sync.dma_start(
                out=out[:, c0 : c0 + 256].rearrange("(m p) n -> p m n", p=P), in_=o_t
            )

        before = {}
        after = {}

        def put(where, index, job, *args):
            where.setdefault(index, []).append((job, args))

        put(before, 0, x_transposes)
        put(after, 0, x_copies)
        put(after, 1, small_vectors)
        put(after, 1, x_codes)
        put(after, 1, win_transposes, 0)
        for g, index in enumerate((2, 3, 5, 6)):
            put(after, index, win_copies, g)
            if g < 3:
                put(after, (2, 4, 5)[g], win_transposes, g + 1)
        for g, index in enumerate((3, 4, 6, 7)):
            put(before, index, win_codes, g)
            put(before, index, state_passes, g)
        for g, index in enumerate((4, 5, 7, 8)):
            put(before, index, state_out, g)
        for g, index in enumerate((5, 6, 8, 9)):
            put(before, index, state_regroup, g)
            put(after, index, state_codes, g)
        put(after, 7, load_noise)
        put(after, 9, finish_t)
        for nb in range(2):
            put(after, 10, noise_transposes, 0, nb)
        for pair in range(4):
            put(after, 10, open_pair, 0, 1, pair)
            put(after, 11 + pair // 2, end_delta, 0, pair)
        for pair in range(4):
            put(after, 11, open_pair, 0, 0, pair)
            put(after, 13, end_signal, 0, pair)
        for pair in range(4):
            put(after, 14 + pair // 2, store, 0, pair)
        for pair in range(4):
            put(after, 13 + pair // 2, out_transposes, 0, pair)
            put(after, 14 + pair // 2, open_pair, 1, 1, pair)
            put(after, 16 + pair // 2, end_delta, 1, pair)
        for nb in range(2):
            put(after, 12, noise_transposes, 1, nb)
            put(after, 13, noise_out, 1, nb)
        for pair in range(4):
            put(after, 15, open_pair, 1, 0, pair)
        for pair, index in ((0, 20), (1, 20), (2, 21), (3, 21)):
            put(after, index, end_signal, 1, pair)
            put(after, index, out_transposes, 1, pair)
        for pair, index in ((0, 20), (1, 20), (2, 21), (3, 21)):
            put(after, index, store, 1, pair)

        def run(jobs):
            for job, args in jobs:
                job(*args)

        last = len(UNITS) - 1
        product(0)
        for i in range(last + 2):
            run(before.get(i, []))
            if i < last:
                product(i + 1)
            if i <= last:
                scalar_regroup(i)
                regrouped_out(i)
            if i < last:
                tensor_regroup(i + 1)
            if i > 0:
                quantise(i - 1)
            if i < last:
                vector_regroup(i + 1)
            run(after.get(i, []))
